import numpy as np
import ml_dtypes


def mxq(x, axis, fmt="e4m3"):
    dtype, down = {"e4m3": (ml_dtypes.float8_e4m3fn, 7), "e5m2": (ml_dtypes.float8_e5m2, 14)}[fmt]
    v = np.moveaxis(np.asarray(x, np.float32).astype(ml_dtypes.bfloat16).astype(np.float64), axis, -1)
    blocks = v.reshape(v.shape[:-1] + (-1, 32))
    amax = np.abs(blocks).max(-1, keepdims=True)
    byte = np.maximum(np.where(amax > 0, np.frexp(amax)[1] - 1 + 127, 0) - down, 1)
    scale = np.exp2(byte - 127.0)
    codes = (blocks / scale).astype(np.float32).astype(dtype).astype(np.float64)
    return np.moveaxis((codes * scale).reshape(v.shape), -1, axis)


WIDE = False


def mx_kscale(k):
    if not WIDE:
        return np.ones(k)
    levels = np.array([10, -10, 5, -5, 0])
    a = np.random.permutation(np.resize(levels, k // 512 * 4)).reshape(k // 512, 4)
    idx = np.arange(k)
    return np.exp2(a[idx // 512, idx % 128 // 32])


BF16 = ml_dtypes.bfloat16


def bf(x):
    return np.asarray(x, np.float32).astype(BF16)


def f64(x):
    return np.asarray(x).astype(np.float64)


B, C, H, W = 1, 512, 32, 32
HW = H * W
EPS = 1e-5


def layernorm(x, g, b):
    mu = x.mean(-1, keepdims=True)
    var = x.var(-1, keepdims=True)
    return (x - mu) / np.sqrt(var + EPS) * g + b


def setup_inputs():
    s = mx_kscale(HW)
    return {"x_fused": bf(np.random.standard_normal((B, C, HW)) * 1.4 + np.random.standard_normal((B, C, 1)) * 0.5),
            "ln_w": bf((1.0 + 0.1 * np.random.standard_normal(HW)) * s),
            "ln_b": bf(0.1 * np.random.standard_normal(HW) * s),
            "w_qk": bf(np.random.standard_normal((2 * HW, HW)) * np.sqrt(2.0 / HW) / s[None, :])}


def reference(x_fused, ln_w, ln_b, w_qk):
    xn = layernorm(f64(x_fused), f64(ln_w), f64(ln_b))
    qk = mxq(xn, 2, "e4m3") @ mxq(f64(w_qk), 1, "e4m3").T
    q, k = qk[..., :HW], qk[..., HW:]
    att = (mxq(q, 1, "e4m3").transpose(0, 2, 1) @ mxq(k, 1, "e4m3")) * HW ** (-0.5)
    return att

@@ -1,0 +1,257 @@
+from contextlib import ExitStack
+
+import concourse.mybir as mybir
+from concourse.masks import make_identity
+
+F32 = mybir.dt.float32
+BF16 = mybir.dt.bfloat16
+U32 = mybir.dt.uint32
+U8 = mybir.dt.uint8
+FP8X4 = mybir.dt.float8_e4m3fn_x4
+ACT = mybir.ActivationFunctionType
+ALU = mybir.AluOpType
+
+P = 128
+PACK = 4
+BANK = 512
+BANKS = 8
+CH = 512
+HW = 1024
+EPS = 1e-5
+PASSES = HW // (P * PACK)
+W_ROWS = 256
+K_BLOCKS = (4, 5, 6, 7)
+Q_BLOCKS = (0, 1, 2, 3)
+W_ORDER = K_BLOCKS + Q_BLOCKS
+EARLY = 3
+
+FLOPS = 2 * CH * 2 * HW * HW + 2 * HW * HW * CH
+
+
+def tile_cmia_pa_kernel(tc, x_fused, ln_w, ln_b, w_qk, out):
+    nc = tc.nc
+    x_rows = x_fused.flatten_outer_dims().rearrange("(m s) n -> m s n", s=PACK)
+    w_blocks = w_qk.rearrange("(b j a) n -> b j (a n)", j=P, a=2)
+    out_rows = out.flatten_outer_dims()
+
+    with ExitStack() as ctx:
+        ctx.enter_context(tc.manual_schedule())
+        keep = ctx.enter_context(tc.tile_pool(name="keep", bufs=1))
+        stage = ctx.enter_context(tc.tile_pool(name="stage", bufs=3))
+        psum = ctx.enter_context(tc.psum_pool(name="psum", bufs=BANKS))
+
+        gb_rows = keep.tile([P, 2 * P], BF16, name="gb_rows")
+        nc.vector.memset(gb_rows[:], 0.0)
+        nc.scalar.dma_start(out=gb_rows[0:4, :], in_=ln_w.rearrange("(r w) -> r w", r=4))
+        nc.scalar.dma_start(out=gb_rows[4:8, :], in_=ln_b.rearrange("(r w) -> r w", r=4))
+        eps = keep.tile([P, 1], F32, name="eps")
+        nc.vector.memset(eps[:], EPS)
+        ident = keep.tile([P, P], F32, name="ident")
+        make_identity(nc, ident[:])
+
+        x_sb = []
+        for s in range(PACK):
+            x_s = keep.tile([P, HW], BF16, name="x_sb%d" % s)
+            nc.sync.dma_start(out=x_s[:], in_=x_rows[:, s, :])
+            x_sb.append(x_s)
+        w_sb = {}
+        for b in W_ORDER:
+            w_b = keep.tile([P, 2 * HW], BF16, name="w_sb%d" % b)
+            nc.sync.dma_start(out=w_b[:], in_=w_blocks[b])
+            w_sb[b] = w_b
+
+        w_grouped = {}
+        w_codes = {}
+        w_scales = {}
+
+        def transpose_w_block(b):
+            words = w_sb[b][:].bitcast(F32)
+            grouped_w = keep.tile([P, PASSES * W_ROWS * PACK], BF16, name="w_grouped%d" % b, align_bytes=64)
+            grouped_words = grouped_w[:].bitcast(F32)
+            for g in range(PASSES):
+                wt = psum.tile([P, BANK], F32, tag="bank")
+                for a in range(2):
+                    for u in range(2):
+                        first = 512 * a + 256 * g + P * u
+                        nc.tensor.transpose(
+                            wt[:, (2 * a + u) * P : (2 * a + u + 1) * P], words[:, first : first + P], ident[:]
+                        )
+                nc.scalar.copy(
+                    out=grouped_words[:, BANK * g : BANK * (g + 1)].rearrange("p (j a u) -> p j a u", a=2, u=2),
+                    in_=wt[:].rearrange("p (a u j) -> p j a u", a=2, u=2),
+                )
+            w_grouped[b] = grouped_w
+
+        def quantise_w_block(b):
+            codes_w = keep.tile([P, PASSES * W_ROWS], U32, name="w_codes%d" % b, align_bytes=64)
+            scales_w = keep.tile([P, PASSES * W_ROWS], U8, name="w_scales%d" % b, align_bytes=64)
+            nc.vector.quantize_mx(out=codes_w[:].bitcast(FP8X4), scales=scales_w[:], in_=w_grouped[b][:])
+            w_codes[b] = codes_w
+            w_scales[b] = scales_w
+
+        mean_var = keep.tile([P, PACK, 2], F32, name="mean_var")
+        std = keep.tile([P, PACK], F32, name="std")
+        rstd = keep.tile([P, PACK], F32, name="rstd")
+        y_sb = []
+
+        def statistics(s):
+            stats = keep.tile([P, 2, 6], F32, name="stats%d" % s)
+            for h in range(2):
+                nc.vector.bn_stats(out=stats[:, h, :], in_=x_sb[s][:, h * 512 : (h + 1) * 512])
+            nc.vector.bn_aggr(out=mean_var[:, s, :], in_=stats[:].rearrange("p h d -> p (h d)"))
+            nc.scalar.activation(
+                out=std[:, s : s + 1], in_=mean_var[:, s, 1:2], func=ACT.Sqrt, bias=eps[:], scale=1.0
+            )
+
+        def normalise(s):
+            nc.vector.reciprocal(out=rstd[:, s : s + 1], in_=std[:, s : s + 1])
+            y_s = keep.tile([P, 4, 2, P], F32, name="y_sb%d" % s)
+            nc.gpsimd.tensor_scalar(
+                out=y_s[:],
+                in0=x_sb[s][:].rearrange("p (r q e) -> p r e q", q=P, e=2),
+                scalar1=mean_var[:, s, 0:1],
+                scalar2=rstd[:, s : s + 1],
+                op0=ALU.subtract,
+                op1=ALU.mult,
+            )
+            y_sb.append(y_s)
+
+        for s in range(PACK):
+            statistics(s)
+            if s >= 1:
+                normalise(s - 1)
+            if s >= 2:
+                transpose_w_block(W_ORDER[s - 2])
+        normalise(PACK - 1)
+        transpose_w_block(W_ORDER[EARLY - 1])
+        for b in W_ORDER[: EARLY - 1]:
+            quantise_w_block(b)
+
+        gb_ps = psum.tile([P, BANK], F32, tag="bank")
+        nc.tensor.transpose(gb_ps[:, 0:P], gb_rows[:].bitcast(F32), ident[:])
+        gb = keep.tile([P, 16], F32, name="gb")
+        nc.vector.tensor_copy(out=gb[:], in_=gb_ps[:].bitcast(BF16)[:, 0:16])
+
+        xn_grouped = []
+        for g in range(PASSES):
+            planes = keep.tile([P, PACK, CH], BF16, name="xn_planes%d" % g)
+            for t in range(PACK):
+                u, e = divmod(t, 2)
+                xt = psum.tile([P, BANK], F32, tag="bank")
+                for s in range(PACK):
+                    nc.tensor.transpose(xt[:, s * P : (s + 1) * P], y_sb[s][:, 2 * g + u, e, :], ident[:])
+                col = PACK * g + t
+                if t % 2 == 0:
+                    nc.scalar.activation(
+                        out=planes[:, t, :],
+                        in_=xt[:],
+                        func=ACT.Identity,
+                        bias=gb[:, 8 + col : 9 + col],
+                        scale=gb[:, col : col + 1],
+                    )
+                else:
+                    nc.vector.tensor_scalar(
+                        out=planes[:, t, :],
+                        in0=xt[:],
+                        scalar1=gb[:, col : col + 1],
+                        scalar2=gb[:, 8 + col : 9 + col],
+                        op0=ALU.mult,
+                        op1=ALU.add,
+                    )
+            grouped = keep.tile([P, CH, PACK], BF16, name="xn_grouped%d" % g, align_bytes=64)
+            nc.vector.tensor_copy(
+                out=grouped[:].rearrange("p (c i) t -> p c t i", i=4),
+                in_=planes[:].rearrange("p t (c i) -> p c t i", i=4),
+            )
+            xn_grouped.append(grouped)
+
+        for b in W_ORDER[EARLY:]:
+            transpose_w_block(b)
+
+        xn_codes = []
+        xn_scales = []
+        for g in range(PASSES):
+            codes = keep.tile([P, CH], U32, name="xn_codes%d" % g, align_bytes=64)
+            scales = keep.tile([P, CH], U8, name="xn_scales%d" % g, align_bytes=64)
+            nc.vector.quantize_mx(
+                out=codes[:].bitcast(FP8X4), scales=scales[:], in_=xn_grouped[g][:].rearrange("p c t -> p (c t)")
+            )
+            xn_codes.append(codes)
+            xn_scales.append(scales)
+        for b in W_ORDER[EARLY - 1 : len(K_BLOCKS)]:
+            quantise_w_block(b)
+
+        def project(b, h, grouped_out):
+            acc = psum.tile([P, BANK], F32, tag="bank")
+            for s in range(PACK):
+                for g in range(PASSES):
+                    cols = slice(W_ROWS * g + P * h, W_ROWS * g + P * (h + 1))
+                    nc.tensor.matmul_mx(
+                        out=acc[:, s * P : (s + 1) * P],
+                        lhsT=xn_codes[g][:, s * P : (s + 1) * P].bitcast(FP8X4),
+                        lhsT_scale=xn_scales[g][:, s * P : (s + 1) * P],
+                        rhs=w_codes[b][:, cols].bitcast(FP8X4),
+                        rhs_scale=w_scales[b][:, cols],
+                        start=(g == 0),
+                        stop=(g == PASSES - 1),
+                    )
+            nc.scalar.copy(out=grouped_out, in_=acc[:].rearrange("p (s j) -> p j s", s=PACK))
+
+        k_codes = []
+        k_scales = []
+        for half in range(2):
+            k_grouped = keep.tile([P, BANK, PACK], BF16, name="k_grouped%d" % half, align_bytes=64)
+            for i in range(2):
+                for h in range(2):
+                    first = W_ROWS * i + P * h
+                    project(K_BLOCKS[2 * half + i], h, k_grouped[:, first : first + P, :])
+                quantise_w_block(Q_BLOCKS[2 * half + i])
+            codes_k = keep.tile([P, BANK], U32, name="k_codes%d" % half, align_bytes=64)
+            scales_k = keep.tile([P, BANK], U8, name="k_scales%d" % half, align_bytes=64)
+            nc.vector.quantize_mx(
+                out=codes_k[:].bitcast(FP8X4), scales=scales_k[:], in_=k_grouped[:].rearrange("p j s -> p (j s)")
+            )
+            k_codes.append(codes_k)
+            k_scales.append(scales_k)
+
+        q_codes = {}
+        q_scales = {}
+
+        def project_q(b):
+            q_grouped = stage.tile([P, W_ROWS, PACK], BF16, tag="q_grouped", align_bytes=64)
+            for h in range(2):
+                project(b, h, q_grouped[:, P * h : P * (h + 1), :])
+            codes_q = stage.tile([P, W_ROWS], U32, tag="q_codes", align_bytes=64)
+            scales_q = stage.tile([P, W_ROWS], U8, tag="q_scales", align_bytes=64)
+            nc.vector.quantize_mx(
+                out=codes_q[:].bitcast(FP8X4), scales=scales_q[:], in_=q_grouped[:].rearrange("p j s -> p (j s)")
+            )
+            q_codes[b] = codes_q
+            q_scales[b] = scales_q
+
+        def attention(b):
+            for h in range(2):
+                att_sb = stage.tile([P, HW], F32, tag="att_sb")
+                for half in range(2):
+                    att = psum.tile([P, BANK], F32, tag="bank")
+                    nc.tensor.matmul_mx(
+                        out=att[:],
+                        lhsT=q_codes[b][:, P * h : P * (h + 1)].bitcast(FP8X4),
+                        lhsT_scale=q_scales[b][:, P * h : P * (h + 1)],
+                        rhs=k_codes[half][:].bitcast(FP8X4),
+                        rhs_scale=k_scales[half][:],
+                        start=True,
+                        stop=True,
+                    )
+                    if half == 0:
+                        nc.scalar.mul(out=att_sb[:, 0:BANK], in_=att[:], mul=HW**-0.5)
+                    else:
+                        nc.vector.tensor_scalar_mul(out=att_sb[:, BANK : 2 * BANK], in0=att[:], scalar1=HW**-0.5)
+                first_row = W_ROWS * b + P * h
+                nc.sync.dma_start(out=out_rows[first_row : first_row + P, :], in_=att_sb[:])
+
+        project_q(Q_BLOCKS[0])
+        for i in range(1, len(Q_BLOCKS)):
+            project_q(Q_BLOCKS[i])
+            attention(Q_BLOCKS[i - 1])
+        attention(Q_BLOCKS[-1])

@@ -92,6 +92,7 @@ def tile_cmia_pa_kernel(tc, x_fused, ln_w, ln_b, w_qk, out):
         mean_var = keep.tile([P, PACK, 2], F32, name="mean_var")
         std = keep.tile([P, PACK], F32, name="std")
         rstd = keep.tile([P, PACK], F32, name="rstd")
+        shift = keep.tile([P, PACK], F32, name="shift")
         y_sb = []
 
         def statistics(s):
@@ -105,14 +106,22 @@ def tile_cmia_pa_kernel(tc, x_fused, ln_w, ln_b, w_qk, out):
 
         def normalise(s):
             nc.vector.reciprocal(out=rstd[:, s : s + 1], in_=std[:, s : s + 1])
+            nc.vector.tensor_scalar(
+                out=shift[:, s : s + 1],
+                in0=mean_var[:, s, 0:1],
+                scalar1=rstd[:, s : s + 1],
+                scalar2=-1.0,
+                op0=ALU.mult,
+                op1=ALU.mult,
+            )
             y_s = keep.tile([P, 4, 2, P], F32, name="y_sb%d" % s)
             nc.gpsimd.tensor_scalar(
                 out=y_s[:],
                 in0=x_sb[s][:].rearrange("p (r q e) -> p r e q", q=P, e=2),
-                scalar1=mean_var[:, s, 0:1],
-                scalar2=rstd[:, s : s + 1],
-                op0=ALU.subtract,
-                op1=ALU.mult,
+                scalar1=rstd[:, s : s + 1],
+                scalar2=shift[:, s : s + 1],
+                op0=ALU.mult,
+                op1=ALU.add,
             )
             y_sb.append(y_s)
 

@@ -23,7 +23,7 @@ W_ROWS = 256
 K_BLOCKS = (4, 5, 6, 7)
 Q_BLOCKS = (0, 1, 2, 3)
 W_ORDER = K_BLOCKS + Q_BLOCKS
-EARLY = 3
+EARLY = 5
 
 FLOPS = 2 * CH * 2 * HW * HW + 2 * HW * HW * CH
 
@@ -37,7 +37,8 @@ def tile_cmia_pa_kernel(tc, x_fused, ln_w, ln_b, w_qk, out):
     with ExitStack() as ctx:
         ctx.enter_context(tc.manual_schedule())
         keep = ctx.enter_context(tc.tile_pool(name="keep", bufs=1))
-        stage = ctx.enter_context(tc.tile_pool(name="stage", bufs=3))
+        stage = ctx.enter_context(tc.tile_pool(name="stage", bufs=4))
+        store = ctx.enter_context(tc.tile_pool(name="store", bufs=6))
         psum = ctx.enter_context(tc.psum_pool(name="psum", bufs=BANKS))
 
         gb_rows = keep.tile([P, 2 * P], BF16, name="gb_rows")
@@ -93,16 +94,8 @@ def tile_cmia_pa_kernel(tc, x_fused, ln_w, ln_b, w_qk, out):
         std = keep.tile([P, PACK], F32, name="std")
         rstd = keep.tile([P, PACK], F32, name="rstd")
         shift = keep.tile([P, PACK], F32, name="shift")
+        stats = keep.tile([P, PACK, 2, 6], F32, name="stats")
         y_sb = []
-
-        def statistics(s):
-            stats = keep.tile([P, 2, 6], F32, name="stats%d" % s)
-            for h in range(2):
-                nc.vector.bn_stats(out=stats[:, h, :], in_=x_sb[s][:, h * 512 : (h + 1) * 512])
-            nc.vector.bn_aggr(out=mean_var[:, s, :], in_=stats[:].rearrange("p h d -> p (h d)"))
-            nc.scalar.activation(
-                out=std[:, s : s + 1], in_=mean_var[:, s, 1:2], func=ACT.Sqrt, bias=eps[:], scale=1.0
-            )
 
         def normalise(s):
             nc.vector.reciprocal(out=rstd[:, s : s + 1], in_=std[:, s : s + 1])
@@ -126,14 +119,20 @@ def tile_cmia_pa_kernel(tc, x_fused, ln_w, ln_b, w_qk, out):
             y_sb.append(y_s)
 
         for s in range(PACK):
-            statistics(s)
+            nc.vector.bn_stats(out=stats[:, s, 0, :], in_=x_sb[s][:, 0:512])
             if s >= 1:
                 normalise(s - 1)
-            if s >= 2:
-                transpose_w_block(W_ORDER[s - 2])
+            nc.vector.bn_stats(out=stats[:, s, 1, :], in_=x_sb[s][:, 512:1024])
+            nc.vector.bn_aggr(out=mean_var[:, s, :], in_=stats[:, s, :, :].rearrange("p h d -> p (h d)"))
+            nc.scalar.activation(
+                out=std[:, s : s + 1], in_=mean_var[:, s, 1:2], func=ACT.Sqrt, bias=eps[:], scale=1.0
+            )
+            if s >= 1:
+                transpose_w_block(W_ORDER[s - 1])
         normalise(PACK - 1)
-        transpose_w_block(W_ORDER[EARLY - 1])
-        for b in W_ORDER[: EARLY - 1]:
+        for b in W_ORDER[PACK - 1 : EARLY]:
+            transpose_w_block(b)
+        for b in W_ORDER[: PACK - 1]:
             quantise_w_block(b)
 
         gb_ps = psum.tile([P, BANK], F32, tag="bank")
@@ -187,10 +186,10 @@ def tile_cmia_pa_kernel(tc, x_fused, ln_w, ln_b, w_qk, out):
             )
             xn_codes.append(codes)
             xn_scales.append(scales)
-        for b in W_ORDER[EARLY - 1 : len(K_BLOCKS)]:
+        for b in W_ORDER[PACK - 1 : len(K_BLOCKS)]:
             quantise_w_block(b)
 
-        def project(b, h, grouped_out):
+        def project(b, h, grouped_out, on_scalar):
             acc = psum.tile([P, BANK], F32, tag="bank")
             for s in range(PACK):
                 for g in range(PASSES):
@@ -204,7 +203,10 @@ def tile_cmia_pa_kernel(tc, x_fused, ln_w, ln_b, w_qk, out):
                         start=(g == 0),
                         stop=(g == PASSES - 1),
                     )
-            nc.scalar.copy(out=grouped_out, in_=acc[:].rearrange("p (s j) -> p j s", s=PACK))
+            if on_scalar:
+                nc.scalar.copy(out=grouped_out, in_=acc[:].rearrange("p (s j) -> p j s", s=PACK))
+            else:
+                nc.vector.tensor_copy(out=grouped_out, in_=acc[:].rearrange("p (s j) -> p j s", s=PACK))
 
         k_codes = []
         k_scales = []
@@ -213,7 +215,7 @@ def tile_cmia_pa_kernel(tc, x_fused, ln_w, ln_b, w_qk, out):
             for i in range(2):
                 for h in range(2):
                     first = W_ROWS * i + P * h
-                    project(K_BLOCKS[2 * half + i], h, k_grouped[:, first : first + P, :])
+                    project(K_BLOCKS[2 * half + i], h, k_grouped[:, first : first + P, :], True)
                 quantise_w_block(Q_BLOCKS[2 * half + i])
             codes_k = keep.tile([P, BANK], U32, name="k_codes%d" % half, align_bytes=64)
             scales_k = keep.tile([P, BANK], U8, name="k_scales%d" % half, align_bytes=64)
@@ -223,44 +225,45 @@ def tile_cmia_pa_kernel(tc, x_fused, ln_w, ln_b, w_qk, out):
             k_codes.append(codes_k)
             k_scales.append(scales_k)
 
-        q_codes = {}
-        q_scales = {}
+        q_codes = []
+        q_scales = []
 
-        def project_q(b):
-            q_grouped = stage.tile([P, W_ROWS, PACK], BF16, tag="q_grouped", align_bytes=64)
-            for h in range(2):
-                project(b, h, q_grouped[:, P * h : P * (h + 1), :])
-            codes_q = stage.tile([P, W_ROWS], U32, tag="q_codes", align_bytes=64)
-            scales_q = stage.tile([P, W_ROWS], U8, tag="q_scales", align_bytes=64)
+        def project_q(unit):
+            b, h = divmod(unit, 2)
+            q_grouped = stage.tile([P, P, PACK], BF16, tag="q_grouped", align_bytes=64)
+            project(Q_BLOCKS[b], h, q_grouped[:], unit % 2 == 0)
+            codes_q = stage.tile([P, P], U32, tag="q_codes", align_bytes=64)
+            scales_q = stage.tile([P, P], U8, tag="q_scales", align_bytes=64)
             nc.vector.quantize_mx(
                 out=codes_q[:].bitcast(FP8X4), scales=scales_q[:], in_=q_grouped[:].rearrange("p j s -> p (j s)")
             )
-            q_codes[b] = codes_q
-            q_scales[b] = scales_q
+            q_codes.append(codes_q)
+            q_scales.append(scales_q)
 
-        def attention(b):
-            for h in range(2):
-                att_sb = stage.tile([P, HW], F32, tag="att_sb")
-                for half in range(2):
-                    att = psum.tile([P, BANK], F32, tag="bank")
-                    nc.tensor.matmul_mx(
-                        out=att[:],
-                        lhsT=q_codes[b][:, P * h : P * (h + 1)].bitcast(FP8X4),
-                        lhsT_scale=q_scales[b][:, P * h : P * (h + 1)],
-                        rhs=k_codes[half][:].bitcast(FP8X4),
-                        rhs_scale=k_scales[half][:],
-                        start=True,
-                        stop=True,
-                    )
-                    if half == 0:
-                        nc.scalar.mul(out=att_sb[:, 0:BANK], in_=att[:], mul=HW**-0.5)
-                    else:
-                        nc.vector.tensor_scalar_mul(out=att_sb[:, BANK : 2 * BANK], in0=att[:], scalar1=HW**-0.5)
-                first_row = W_ROWS * b + P * h
-                nc.sync.dma_start(out=out_rows[first_row : first_row + P, :], in_=att_sb[:])
+        def attention(unit):
+            for half in range(2):
+                att = psum.tile([P, BANK], F32, tag="bank")
+                nc.tensor.matmul_mx(
+                    out=att[:],
+                    lhsT=q_codes[unit][:].bitcast(FP8X4),
+                    lhsT_scale=q_scales[unit][:],
+                    rhs=k_codes[half][:].bitcast(FP8X4),
+                    rhs_scale=k_scales[half][:],
+                    start=True,
+                    stop=True,
+                )
+                att_sb = store.tile([P, BANK], F32, tag="att_sb")
+                if half == 0:
+                    nc.scalar.mul(out=att_sb[:], in_=att[:], mul=HW**-0.5)
+                else:
+                    nc.vector.tensor_scalar_mul(out=att_sb[:], in0=att[:], scalar1=HW**-0.5)
+                nc.sync.dma_start(
+                    out=out_rows[P * unit : P * (unit + 1), BANK * half : BANK * (half + 1)], in_=att_sb[:]
+                )
 
-        project_q(Q_BLOCKS[0])
-        for i in range(1, len(Q_BLOCKS)):
-            project_q(Q_BLOCKS[i])
-            attention(Q_BLOCKS[i - 1])
-        attention(Q_BLOCKS[-1])
+        units = HW // P
+        project_q(0)
+        for unit in range(1, units):
+            project_q(unit)
+            attention(unit - 1)
+        attention(units - 1)

@@ -23,7 +23,8 @@ W_ROWS = 256
 K_BLOCKS = (4, 5, 6, 7)
 Q_BLOCKS = (0, 1, 2, 3)
 W_ORDER = K_BLOCKS + Q_BLOCKS
-EARLY = 5
+EARLY = 4
+LAG = 2
 
 FLOPS = 2 * CH * 2 * HW * HW + 2 * HW * HW * CH
 
@@ -95,52 +96,71 @@ def tile_cmia_pa_kernel(tc, x_fused, ln_w, ln_b, w_qk, out):
         rstd = keep.tile([P, PACK], F32, name="rstd")
         shift = keep.tile([P, PACK], F32, name="shift")
         stats = keep.tile([P, PACK, 2, 6], F32, name="stats")
-        y_sb = []
+        y_sb = [keep.tile([P, 4, 2, P], F32, name="y_sb%d" % s) for s in range(PACK)]
 
-        def normalise(s):
-            nc.vector.reciprocal(out=rstd[:, s : s + 1], in_=std[:, s : s + 1])
-            nc.vector.tensor_scalar(
-                out=shift[:, s : s + 1],
-                in0=mean_var[:, s, 0:1],
-                scalar1=rstd[:, s : s + 1],
-                scalar2=-1.0,
-                op0=ALU.mult,
-                op1=ALU.mult,
-            )
-            y_s = keep.tile([P, 4, 2, P], F32, name="y_sb%d" % s)
-            nc.gpsimd.tensor_scalar(
-                out=y_s[:],
-                in0=x_sb[s][:].rearrange("p (r q e) -> p r e q", q=P, e=2),
-                scalar1=rstd[:, s : s + 1],
-                scalar2=shift[:, s : s + 1],
-                op0=ALU.mult,
-                op1=ALU.add,
-            )
-            y_sb.append(y_s)
+        def by_parity(s):
+            return x_sb[s][:].rearrange("p (r q e) -> p r e q", q=P, e=2)
 
         for s in range(PACK):
             nc.vector.bn_stats(out=stats[:, s, 0, :], in_=x_sb[s][:, 0:512])
             if s >= 1:
-                normalise(s - 1)
+                nc.vector.reciprocal(out=rstd[:, s - 1 : s], in_=std[:, s - 1 : s])
             nc.vector.bn_stats(out=stats[:, s, 1, :], in_=x_sb[s][:, 512:1024])
+            if s >= 1:
+                nc.vector.tensor_scalar(
+                    out=shift[:, s - 1 : s],
+                    in0=mean_var[:, s - 1, 0:1],
+                    scalar1=rstd[:, s - 1 : s],
+                    scalar2=-1.0,
+                    op0=ALU.mult,
+                    op1=ALU.mult,
+                )
+                nc.gpsimd.tensor_scalar(
+                    out=y_sb[s - 1][:],
+                    in0=by_parity(s - 1),
+                    scalar1=rstd[:, s - 1 : s],
+                    scalar2=shift[:, s - 1 : s],
+                    op0=ALU.mult,
+                    op1=ALU.add,
+                )
             nc.vector.bn_aggr(out=mean_var[:, s, :], in_=stats[:, s, :, :].rearrange("p h d -> p (h d)"))
             nc.scalar.activation(
                 out=std[:, s : s + 1], in_=mean_var[:, s, 1:2], func=ACT.Sqrt, bias=eps[:], scale=1.0
             )
             if s >= 1:
                 transpose_w_block(W_ORDER[s - 1])
-        normalise(PACK - 1)
-        for b in W_ORDER[PACK - 1 : EARLY]:
-            transpose_w_block(b)
-        for b in W_ORDER[: PACK - 1]:
-            quantise_w_block(b)
-
+        last = PACK - 1
+        nc.vector.reciprocal(out=rstd[:, last : last + 1], in_=std[:, last : last + 1])
+        nc.vector.tensor_scalar(
+            out=y_sb[last][:],
+            in0=by_parity(last),
+            scalar1=mean_var[:, last, 0:1],
+            scalar2=rstd[:, last : last + 1],
+            op0=ALU.subtract,
+            op1=ALU.mult,
+        )
         gb_ps = psum.tile([P, BANK], F32, tag="bank")
         nc.tensor.transpose(gb_ps[:, 0:P], gb_rows[:].bitcast(F32), ident[:])
         gb = keep.tile([P, 16], F32, name="gb")
-        nc.vector.tensor_copy(out=gb[:], in_=gb_ps[:].bitcast(BF16)[:, 0:16])
+        nc.scalar.copy(out=gb[:], in_=gb_ps[:].bitcast(BF16)[:, 0:16])
+
+        for b in W_ORDER[PACK - 1 : EARLY]:
+            transpose_w_block(b)
+        quantise_w_block(W_ORDER[0])
 
         xn_grouped = []
+        xn_codes = []
+        xn_scales = []
+
+        def quantise_xn(g):
+            codes = keep.tile([P, CH], U32, name="xn_codes%d" % g, align_bytes=64)
+            scales = keep.tile([P, CH], U8, name="xn_scales%d" % g, align_bytes=64)
+            nc.vector.quantize_mx(
+                out=codes[:].bitcast(FP8X4), scales=scales[:], in_=xn_grouped[g][:].rearrange("p c t -> p (c t)")
+            )
+            xn_codes.append(codes)
+            xn_scales.append(scales)
+
         for g in range(PASSES):
             planes = keep.tile([P, PACK, CH], BF16, name="xn_planes%d" % g)
             for t in range(PACK):
@@ -166,6 +186,8 @@ def tile_cmia_pa_kernel(tc, x_fused, ln_w, ln_b, w_qk, out):
                         op0=ALU.mult,
                         op1=ALU.add,
                     )
+                if g >= 1 and t == 1:
+                    quantise_xn(g - 1)
             grouped = keep.tile([P, CH, PACK], BF16, name="xn_grouped%d" % g, align_bytes=64)
             nc.vector.tensor_copy(
                 out=grouped[:].rearrange("p (c i) t -> p c t i", i=4),
@@ -175,18 +197,8 @@ def tile_cmia_pa_kernel(tc, x_fused, ln_w, ln_b, w_qk, out):
 
         for b in W_ORDER[EARLY:]:
             transpose_w_block(b)
-
-        xn_codes = []
-        xn_scales = []
-        for g in range(PASSES):
-            codes = keep.tile([P, CH], U32, name="xn_codes%d" % g, align_bytes=64)
-            scales = keep.tile([P, CH], U8, name="xn_scales%d" % g, align_bytes=64)
-            nc.vector.quantize_mx(
-                out=codes[:].bitcast(FP8X4), scales=scales[:], in_=xn_grouped[g][:].rearrange("p c t -> p (c t)")
-            )
-            xn_codes.append(codes)
-            xn_scales.append(scales)
-        for b in W_ORDER[PACK - 1 : len(K_BLOCKS)]:
+        quantise_xn(PASSES - 1)
+        for b in W_ORDER[1:]:
             quantise_w_block(b)
 
         def project(b, h, grouped_out, on_scalar):
@@ -216,7 +228,6 @@ def tile_cmia_pa_kernel(tc, x_fused, ln_w, ln_b, w_qk, out):
                 for h in range(2):
                     first = W_ROWS * i + P * h
                     project(K_BLOCKS[2 * half + i], h, k_grouped[:, first : first + P, :], True)
-                quantise_w_block(Q_BLOCKS[2 * half + i])
             codes_k = keep.tile([P, BANK], U32, name="k_codes%d" % half, align_bytes=64)
             scales_k = keep.tile([P, BANK], U8, name="k_scales%d" % half, align_bytes=64)
             nc.vector.quantize_mx(
@@ -262,8 +273,8 @@ def tile_cmia_pa_kernel(tc, x_fused, ln_w, ln_b, w_qk, out):
                 )
 
         units = HW // P
-        project_q(0)
-        for unit in range(1, units):
-            project_q(unit)
-            attention(unit - 1)
-        attention(units - 1)
+        for unit in range(units + LAG):
+            if unit < units:
+                project_q(unit)
+            if unit >= LAG:
+                attention(unit - LAG)

@@ -23,7 +23,7 @@ W_ROWS = 256
 K_BLOCKS = (4, 5, 6, 7)
 Q_BLOCKS = (0, 1, 2, 3)
 W_ORDER = K_BLOCKS + Q_BLOCKS
-EARLY = 4
+NORMALISED = (0, 2, 3, 1)
 LAG = 2
 
 FLOPS = 2 * CH * 2 * HW * HW + 2 * HW * HW * CH
@@ -38,8 +38,8 @@ def tile_cmia_pa_kernel(tc, x_fused, ln_w, ln_b, w_qk, out):
     with ExitStack() as ctx:
         ctx.enter_context(tc.manual_schedule())
         keep = ctx.enter_context(tc.tile_pool(name="keep", bufs=1))
-        stage = ctx.enter_context(tc.tile_pool(name="stage", bufs=4))
-        store = ctx.enter_context(tc.tile_pool(name="store", bufs=6))
+        stage = ctx.enter_context(tc.tile_pool(name="stage", bufs=8))
+        store = ctx.enter_context(tc.tile_pool(name="store", bufs=16))
         psum = ctx.enter_context(tc.psum_pool(name="psum", bufs=BANKS))
 
         gb_rows = keep.tile([P, 2 * P], BF16, name="gb_rows")
@@ -48,6 +48,8 @@ def tile_cmia_pa_kernel(tc, x_fused, ln_w, ln_b, w_qk, out):
         nc.scalar.dma_start(out=gb_rows[4:8, :], in_=ln_b.rearrange("(r w) -> r w", r=4))
         eps = keep.tile([P, 1], F32, name="eps")
         nc.vector.memset(eps[:], EPS)
+        first_root = keep.tile([P, 1], F32, name="first_root")
+        nc.scalar.activation(out=first_root[:], in_=eps[:], func=ACT.Abs_reciprocal_sqrt)
         ident = keep.tile([P, P], F32, name="ident")
         make_identity(nc, ident[:])
 
@@ -66,23 +68,34 @@ def tile_cmia_pa_kernel(tc, x_fused, ln_w, ln_b, w_qk, out):
         w_codes = {}
         w_scales = {}
 
-        def transpose_w_block(b):
+        def copy_out(dst, src, on_scalar):
+            if on_scalar:
+                nc.scalar.copy(out=dst, in_=src)
+            else:
+                nc.vector.tensor_copy(out=dst, in_=src)
+
+        w_banks = {}
+
+        def transpose_w(b, g):
             words = w_sb[b][:].bitcast(F32)
-            grouped_w = keep.tile([P, PASSES * W_ROWS * PACK], BF16, name="w_grouped%d" % b, align_bytes=64)
-            grouped_words = grouped_w[:].bitcast(F32)
-            for g in range(PASSES):
-                wt = psum.tile([P, BANK], F32, tag="bank")
-                for a in range(2):
-                    for u in range(2):
-                        first = 512 * a + 256 * g + P * u
-                        nc.tensor.transpose(
-                            wt[:, (2 * a + u) * P : (2 * a + u + 1) * P], words[:, first : first + P], ident[:]
-                        )
-                nc.scalar.copy(
-                    out=grouped_words[:, BANK * g : BANK * (g + 1)].rearrange("p (j a u) -> p j a u", a=2, u=2),
-                    in_=wt[:].rearrange("p (a u j) -> p j a u", a=2, u=2),
-                )
-            w_grouped[b] = grouped_w
+            wt = psum.tile([P, BANK], F32, tag="bank")
+            for a in range(2):
+                for u in range(2):
+                    first = 512 * a + 256 * g + P * u
+                    nc.tensor.transpose(
+                        wt[:, (2 * a + u) * P : (2 * a + u + 1) * P], words[:, first : first + P], ident[:]
+                    )
+            w_banks[b, g] = wt
+
+        def group_w(b, g, on_scalar=True):
+            if g == 0:
+                w_grouped[b] = keep.tile([P, PASSES * W_ROWS * PACK], BF16, name="w_grouped%d" % b, align_bytes=64)
+            grouped_words = w_grouped[b][:].bitcast(F32)[:, BANK * g : BANK * (g + 1)]
+            copy_out(
+                grouped_words.rearrange("p (j a u) -> p j a u", a=2, u=2),
+                w_banks[b, g][:].rearrange("p (a u j) -> p j a u", a=2, u=2),
+                on_scalar,
+            )
 
         def quantise_w_block(b):
             codes_w = keep.tile([P, PASSES * W_ROWS], U32, name="w_codes%d" % b, align_bytes=64)
@@ -92,7 +105,6 @@ def tile_cmia_pa_kernel(tc, x_fused, ln_w, ln_b, w_qk, out):
             w_scales[b] = scales_w
 
         mean_var = keep.tile([P, PACK, 2], F32, name="mean_var")
-        std = keep.tile([P, PACK], F32, name="std")
         rstd = keep.tile([P, PACK], F32, name="rstd")
         shift = keep.tile([P, PACK], F32, name="shift")
         stats = keep.tile([P, PACK, 2, 6], F32, name="stats")
@@ -101,107 +113,143 @@ def tile_cmia_pa_kernel(tc, x_fused, ln_w, ln_b, w_qk, out):
         def by_parity(s):
             return x_sb[s][:].rearrange("p (r q e) -> p r e q", q=P, e=2)
 
-        for s in range(PACK):
-            nc.vector.bn_stats(out=stats[:, s, 0, :], in_=x_sb[s][:, 0:512])
-            if s >= 1:
-                nc.vector.reciprocal(out=rstd[:, s - 1 : s], in_=std[:, s - 1 : s])
-            nc.vector.bn_stats(out=stats[:, s, 1, :], in_=x_sb[s][:, 512:1024])
-            if s >= 1:
-                nc.vector.tensor_scalar(
-                    out=shift[:, s - 1 : s],
-                    in0=mean_var[:, s - 1, 0:1],
-                    scalar1=rstd[:, s - 1 : s],
-                    scalar2=-1.0,
-                    op0=ALU.mult,
-                    op1=ALU.mult,
-                )
-                nc.gpsimd.tensor_scalar(
-                    out=y_sb[s - 1][:],
-                    in0=by_parity(s - 1),
-                    scalar1=rstd[:, s - 1 : s],
-                    scalar2=shift[:, s - 1 : s],
-                    op0=ALU.mult,
-                    op1=ALU.add,
-                )
+        x_sum = keep.tile([P, 1], F32, name="x_sum")
+        x_sq = keep.tile([P, 1], F32, name="x_sq")
+        neg_mean = keep.tile([P, 1], F32, name="neg_mean")
+        unused = keep.tile([P, HW], BF16, name="unused")
+
+        def half_stats(s, half):
+            nc.vector.bn_stats(out=stats[:, s, half, :], in_=x_sb[s][:, BANK * half : BANK * (half + 1)])
+
+        def join_stats(s):
             nc.vector.bn_aggr(out=mean_var[:, s, :], in_=stats[:, s, :, :].rearrange("p h d -> p (h d)"))
+
+        def invert_root(s, var, scale):
             nc.scalar.activation(
-                out=std[:, s : s + 1], in_=mean_var[:, s, 1:2], func=ACT.Sqrt, bias=eps[:], scale=1.0
+                out=rstd[:, s : s + 1], in_=var, func=ACT.Abs_reciprocal_sqrt, bias=eps[:], scale=scale
             )
-            if s >= 1:
-                transpose_w_block(W_ORDER[s - 1])
-        last = PACK - 1
-        nc.vector.reciprocal(out=rstd[:, last : last + 1], in_=std[:, last : last + 1])
+
+        def normalise_on_gpsimd(s):
+            nc.gpsimd.tensor_scalar(
+                out=y_sb[s][:],
+                in0=by_parity(s),
+                scalar1=rstd[:, s : s + 1],
+                scalar2=shift[:, s : s + 1],
+                op0=ALU.mult,
+                op1=ALU.add,
+            )
+
+        def normalise_on_vector(s):
+            nc.vector.tensor_scalar(
+                out=y_sb[s][:],
+                in0=by_parity(s),
+                scalar1=mean_var[:, s, 0:1],
+                scalar2=rstd[:, s : s + 1],
+                op0=ALU.subtract,
+                op1=ALU.mult,
+            )
+
+        half_stats(0, 0)
+        nc.scalar.activation(out=unused[:], in_=x_sb[1][:], func=ACT.Identity, accum_out=x_sum[:])
+        half_stats(0, 1)
+        join_stats(0)
+        nc.scalar.mul(out=neg_mean[:], in_=x_sum[:], mul=-1.0 / HW)
+        invert_root(0, mean_var[:, 0, 1:2], 1.0)
+        half_stats(2, 0)
+        nc.scalar.activation(
+            out=unused[:], in_=x_sb[1][:], func=ACT.Square, bias=neg_mean[:], scale=1.0, accum_out=x_sq[:]
+        )
         nc.vector.tensor_scalar(
-            out=y_sb[last][:],
-            in0=by_parity(last),
-            scalar1=mean_var[:, last, 0:1],
-            scalar2=rstd[:, last : last + 1],
-            op0=ALU.subtract,
+            out=shift[:, 0:1],
+            in0=mean_var[:, 0, 0:1],
+            scalar1=rstd[:, 0:1],
+            scalar2=-1.0,
+            op0=ALU.mult,
             op1=ALU.mult,
         )
+        normalise_on_gpsimd(0)
+        half_stats(2, 1)
+        join_stats(2)
+        invert_root(1, x_sq[:], 1.0 / HW)
+        invert_root(2, mean_var[:, 2, 1:2], 1.0)
+        nc.scalar.activation(out=shift[:, 1:2], in_=neg_mean[:], func=ACT.Copy, scale=rstd[:, 1:2])
+        normalise_on_gpsimd(1)
+        half_stats(3, 0)
+        transpose_w(K_BLOCKS[0], 0)
+        group_w(K_BLOCKS[0], 0)
+        half_stats(3, 1)
+        join_stats(3)
+        invert_root(3, mean_var[:, 3, 1:2], 1.0)
+        normalise_on_vector(2)
+        normalise_on_vector(3)
+        transpose_w(K_BLOCKS[0], 1)
+        group_w(K_BLOCKS[0], 1)
+        quantise_w_block(K_BLOCKS[0])
+
         gb_ps = psum.tile([P, BANK], F32, tag="bank")
         nc.tensor.transpose(gb_ps[:, 0:P], gb_rows[:].bitcast(F32), ident[:])
         gb = keep.tile([P, 16], F32, name="gb")
         nc.scalar.copy(out=gb[:], in_=gb_ps[:].bitcast(BF16)[:, 0:16])
 
-        for b in W_ORDER[PACK - 1 : EARLY]:
-            transpose_w_block(b)
-        quantise_w_block(W_ORDER[0])
 
-        xn_grouped = []
-        xn_codes = []
-        xn_scales = []
+        xn_codes = [keep.tile([P, CH], U32, name="xn_codes%d" % g, align_bytes=64) for g in range(PASSES)]
+        xn_scales = [keep.tile([P, CH], U8, name="xn_scales%d" % g, align_bytes=64) for g in range(PASSES)]
+        planes = [keep.tile([P, PACK, CH], BF16, name="xn_planes%d" % g) for g in range(PASSES)]
+        grouped = [keep.tile([P, CH, PACK], BF16, name="xn_grouped%d" % g, align_bytes=64) for g in range(PASSES)]
 
-        def quantise_xn(g):
-            codes = keep.tile([P, CH], U32, name="xn_codes%d" % g, align_bytes=64)
-            scales = keep.tile([P, CH], U8, name="xn_scales%d" % g, align_bytes=64)
-            nc.vector.quantize_mx(
-                out=codes[:].bitcast(FP8X4), scales=scales[:], in_=xn_grouped[g][:].rearrange("p c t -> p (c t)")
+        def transpose_xn(bank, g, t, s):
+            u, e = divmod(t, 2)
+            nc.tensor.transpose(bank[:, s * P : (s + 1) * P], y_sb[s][:, 2 * g + u, e, :], ident[:])
+
+        def affine_xn(bank, g, t, on_scalar):
+            col = PACK * g + t
+            gain, bias = gb[:, col : col + 1], gb[:, 8 + col : 9 + col]
+            if on_scalar:
+                nc.scalar.activation(out=planes[g][:, t, :], in_=bank[:], func=ACT.Identity, bias=bias, scale=gain)
+            else:
+                nc.vector.tensor_scalar(
+                    out=planes[g][:, t, :], in0=bank[:], scalar1=gain, scalar2=bias, op0=ALU.mult, op1=ALU.add
+                )
+
+        def interleave_xn(g, first, last):
+            nc.vector.tensor_copy(
+                out=grouped[g][:, first:last, :].rearrange("p (c i) t -> p c t i", i=4),
+                in_=planes[g][:, :, first:last].rearrange("p t (c i) -> p c t i", i=4),
             )
-            xn_codes.append(codes)
-            xn_scales.append(scales)
+
+        def quantise_xn(g, first, last):
+            nc.vector.quantize_mx(
+                out=xn_codes[g][:, first:last].bitcast(FP8X4),
+                scales=xn_scales[g][:, first:last],
+                in_=grouped[g][:, first:last, :].rearrange("p c t -> p (c t)"),
+            )
 
         for g in range(PASSES):
-            planes = keep.tile([P, PACK, CH], BF16, name="xn_planes%d" % g)
+            banks = []
             for t in range(PACK):
-                u, e = divmod(t, 2)
                 xt = psum.tile([P, BANK], F32, tag="bank")
-                for s in range(PACK):
-                    nc.tensor.transpose(xt[:, s * P : (s + 1) * P], y_sb[s][:, 2 * g + u, e, :], ident[:])
-                col = PACK * g + t
-                if t % 2 == 0:
-                    nc.scalar.activation(
-                        out=planes[:, t, :],
-                        in_=xt[:],
-                        func=ACT.Identity,
-                        bias=gb[:, 8 + col : 9 + col],
-                        scale=gb[:, col : col + 1],
-                    )
-                else:
-                    nc.vector.tensor_scalar(
-                        out=planes[:, t, :],
-                        in0=xt[:],
-                        scalar1=gb[:, col : col + 1],
-                        scalar2=gb[:, 8 + col : 9 + col],
-                        op0=ALU.mult,
-                        op1=ALU.add,
-                    )
-                if g >= 1 and t == 1:
-                    quantise_xn(g - 1)
-            grouped = keep.tile([P, CH, PACK], BF16, name="xn_grouped%d" % g, align_bytes=64)
-            nc.vector.tensor_copy(
-                out=grouped[:].rearrange("p (c i) t -> p c t i", i=4),
-                in_=planes[:].rearrange("p t (c i) -> p c t i", i=4),
-            )
-            xn_grouped.append(grouped)
+                banks.append(xt)
+            for s in NORMALISED:
+                for t in range(PACK):
+                    transpose_xn(banks[t], g, t, s)
+            for t in range(PACK):
+                affine_xn(banks[t], g, t, g == 1 or t % 2 == 0)
+            if g == 0:
+                interleave_xn(0, 0, CH)
+                quantise_xn(0, 0, CH)
+        for b in K_BLOCKS[1:]:
+            for g in range(PASSES):
+                transpose_w(b, g)
+                group_w(b, g)
+        for g in range(PASSES):
+            transpose_w(Q_BLOCKS[0], g)
+        interleave_xn(1, 0, CH // 2)
+        interleave_xn(1, CH // 2, CH)
+        quantise_xn(1, 0, CH // 2)
+        quantise_xn(1, CH // 2, CH)
+        quantise_w_block(K_BLOCKS[1])
 
-        for b in W_ORDER[EARLY:]:
-            transpose_w_block(b)
-        quantise_xn(PASSES - 1)
-        for b in W_ORDER[1:]:
-            quantise_w_block(b)
-
-        def project(b, h, grouped_out, on_scalar):
+        def project(b, h):
             acc = psum.tile([P, BANK], F32, tag="bank")
             for s in range(PACK):
                 for g in range(PASSES):
@@ -215,26 +263,45 @@ def tile_cmia_pa_kernel(tc, x_fused, ln_w, ln_b, w_qk, out):
                         start=(g == 0),
                         stop=(g == PASSES - 1),
                     )
-            if on_scalar:
-                nc.scalar.copy(out=grouped_out, in_=acc[:].rearrange("p (s j) -> p j s", s=PACK))
-            else:
-                nc.vector.tensor_copy(out=grouped_out, in_=acc[:].rearrange("p (s j) -> p j s", s=PACK))
+            return acc[:].rearrange("p (s j) -> p j s", s=PACK)
 
-        k_codes = []
-        k_scales = []
-        for half in range(2):
-            k_grouped = keep.tile([P, BANK, PACK], BF16, name="k_grouped%d" % half, align_bytes=64)
-            for i in range(2):
-                for h in range(2):
-                    first = W_ROWS * i + P * h
-                    project(K_BLOCKS[2 * half + i], h, k_grouped[:, first : first + P, :], True)
-            codes_k = keep.tile([P, BANK], U32, name="k_codes%d" % half, align_bytes=64)
-            scales_k = keep.tile([P, BANK], U8, name="k_scales%d" % half, align_bytes=64)
+        k_grouped = [keep.tile([P, BANK, PACK], BF16, name="k_grouped%d" % i, align_bytes=64) for i in range(2)]
+        k_codes = [keep.tile([P, BANK], U32, name="k_codes%d" % i, align_bytes=64) for i in range(2)]
+        k_scales = [keep.tile([P, BANK], U8, name="k_scales%d" % i, align_bytes=64) for i in range(2)]
+
+        def project_k(i, h, on_scalar):
+            half, first = i // 2, W_ROWS * (i % 2) + P * h
+            copy_out(k_grouped[half][:, first : first + P, :], project(K_BLOCKS[i], h), on_scalar)
+
+        def quantise_k(half):
             nc.vector.quantize_mx(
-                out=codes_k[:].bitcast(FP8X4), scales=scales_k[:], in_=k_grouped[:].rearrange("p j s -> p (j s)")
+                out=k_codes[half][:].bitcast(FP8X4),
+                scales=k_scales[half][:],
+                in_=k_grouped[half][:].rearrange("p j s -> p (j s)"),
             )
-            k_codes.append(codes_k)
-            k_scales.append(scales_k)
+
+        def turn_w(b):
+            for g in range(PASSES):
+                transpose_w(b, g)
+                group_w(b, g)
+
+        project_k(0, 0, False)
+        quantise_w_block(K_BLOCKS[2])
+        project_k(0, 1, True)
+        group_w(Q_BLOCKS[0], 0)
+        project_k(1, 0, False)
+        quantise_w_block(K_BLOCKS[3])
+        project_k(1, 1, True)
+        group_w(Q_BLOCKS[0], 1)
+        project_k(2, 0, False)
+        quantise_k(0)
+        quantise_w_block(Q_BLOCKS[0])
+        project_k(2, 1, True)
+        project_k(3, 0, False)
+        project_k(3, 1, True)
+        turn_w(Q_BLOCKS[1])
+        quantise_k(1)
+        quantise_w_block(Q_BLOCKS[1])
 
         q_codes = []
         q_scales = []
@@ -242,7 +309,7 @@ def tile_cmia_pa_kernel(tc, x_fused, ln_w, ln_b, w_qk, out):
         def project_q(unit):
             b, h = divmod(unit, 2)
             q_grouped = stage.tile([P, P, PACK], BF16, tag="q_grouped", align_bytes=64)
-            project(Q_BLOCKS[b], h, q_grouped[:], unit % 2 == 0)
+            copy_out(q_grouped[:], project(Q_BLOCKS[b], h), unit % 2 == 0)
             codes_q = stage.tile([P, P], U32, tag="q_codes", align_bytes=64)
             scales_q = stage.tile([P, P], U8, tag="q_scales", align_bytes=64)
             nc.vector.quantize_mx(
@@ -278,3 +345,6 @@ def tile_cmia_pa_kernel(tc, x_fused, ln_w, ln_b, w_qk, out):
                 project_q(unit)
             if unit >= LAG:
                 attention(unit - LAG)
+            if unit == 1 or unit == 3:
+                turn_w(Q_BLOCKS[(unit + 3) // 2])
+                quantise_w_block(Q_BLOCKS[(unit + 3) // 2])

@@ -23,7 +23,7 @@ W_ROWS = 256
 K_BLOCKS = (4, 5, 6, 7)
 Q_BLOCKS = (0, 1, 2, 3)
 W_ORDER = K_BLOCKS + Q_BLOCKS
-NORMALISED = (0, 2, 3, 1)
+NORMALISED = (0, 2, 1, 3)
 LAG = 2
 
 FLOPS = 2 * CH * 2 * HW * HW + 2 * HW * HW * CH
@@ -106,7 +106,7 @@ def tile_cmia_pa_kernel(tc, x_fused, ln_w, ln_b, w_qk, out):
 
         mean_var = keep.tile([P, PACK, 2], F32, name="mean_var")
         rstd = keep.tile([P, PACK], F32, name="rstd")
-        shift = keep.tile([P, PACK], F32, name="shift")
+        shift = keep.tile([P, 1], F32, name="shift")
         stats = keep.tile([P, PACK, 2, 6], F32, name="stats")
         y_sb = [keep.tile([P, 4, 2, P], F32, name="y_sb%d" % s) for s in range(PACK)]
 
@@ -129,16 +129,6 @@ def tile_cmia_pa_kernel(tc, x_fused, ln_w, ln_b, w_qk, out):
                 out=rstd[:, s : s + 1], in_=var, func=ACT.Abs_reciprocal_sqrt, bias=eps[:], scale=scale
             )
 
-        def normalise_on_gpsimd(s):
-            nc.gpsimd.tensor_scalar(
-                out=y_sb[s][:],
-                in0=by_parity(s),
-                scalar1=rstd[:, s : s + 1],
-                scalar2=shift[:, s : s + 1],
-                op0=ALU.mult,
-                op1=ALU.add,
-            )
-
         def normalise_on_vector(s):
             nc.vector.tensor_scalar(
                 out=y_sb[s][:],
@@ -159,32 +149,25 @@ def tile_cmia_pa_kernel(tc, x_fused, ln_w, ln_b, w_qk, out):
         nc.scalar.activation(
             out=unused[:], in_=x_sb[1][:], func=ACT.Square, bias=neg_mean[:], scale=1.0, accum_out=x_sq[:]
         )
-        nc.vector.tensor_scalar(
-            out=shift[:, 0:1],
-            in0=mean_var[:, 0, 0:1],
-            scalar1=rstd[:, 0:1],
-            scalar2=-1.0,
-            op0=ALU.mult,
-            op1=ALU.mult,
-        )
-        normalise_on_gpsimd(0)
         half_stats(2, 1)
         join_stats(2)
+        normalise_on_vector(0)
         invert_root(1, x_sq[:], 1.0 / HW)
         invert_root(2, mean_var[:, 2, 1:2], 1.0)
-        nc.scalar.activation(out=shift[:, 1:2], in_=neg_mean[:], func=ACT.Copy, scale=rstd[:, 1:2])
-        normalise_on_gpsimd(1)
+        nc.scalar.activation(out=shift[:], in_=neg_mean[:], func=ACT.Copy, scale=rstd[:, 1:2])
         half_stats(3, 0)
         transpose_w(K_BLOCKS[0], 0)
-        group_w(K_BLOCKS[0], 0)
         half_stats(3, 1)
         join_stats(3)
-        invert_root(3, mean_var[:, 3, 1:2], 1.0)
+        nc.scalar.activation(
+            out=y_sb[1][:], in_=by_parity(1), func=ACT.Identity, bias=shift[:], scale=rstd[:, 1:2]
+        )
         normalise_on_vector(2)
+        invert_root(3, mean_var[:, 3, 1:2], 1.0)
         normalise_on_vector(3)
         transpose_w(K_BLOCKS[0], 1)
+        group_w(K_BLOCKS[0], 0)
         group_w(K_BLOCKS[0], 1)
-        quantise_w_block(K_BLOCKS[0])
 
         gb_ps = psum.tile([P, BANK], F32, tag="bank")
         nc.tensor.transpose(gb_ps[:, 0:P], gb_rows[:].bitcast(F32), ident[:])
@@ -237,6 +220,7 @@ def tile_cmia_pa_kernel(tc, x_fused, ln_w, ln_b, w_qk, out):
             if g == 0:
                 interleave_xn(0, 0, CH)
                 quantise_xn(0, 0, CH)
+                quantise_w_block(K_BLOCKS[0])
         for b in K_BLOCKS[1:]:
             for g in range(PASSES):
                 transpose_w(b, g)

@@ -219,8 +219,8 @@ def tile_cmia_pa_kernel(tc, x_fused, ln_w, ln_b, w_qk, out):
                 affine_xn(banks[t], g, t, g == 1 or t % 2 == 0)
             if g == 0:
                 interleave_xn(0, 0, CH)
-                quantise_xn(0, 0, CH)
                 quantise_w_block(K_BLOCKS[0])
+                quantise_xn(0, 0, CH)
         for b in K_BLOCKS[1:]:
             for g in range(PASSES):
                 transpose_w(b, g)
@@ -283,9 +283,13 @@ def tile_cmia_pa_kernel(tc, x_fused, ln_w, ln_b, w_qk, out):
         project_k(2, 1, True)
         project_k(3, 0, False)
         project_k(3, 1, True)
-        turn_w(Q_BLOCKS[1])
-        quantise_k(1)
-        quantise_w_block(Q_BLOCKS[1])
+        for b in Q_BLOCKS[1:]:
+            for g in range(PASSES):
+                transpose_w(b, g)
+                group_w(b, g, b != Q_BLOCKS[2])
+            if b == Q_BLOCKS[1]:
+                quantise_k(1)
+                quantise_w_block(b)
 
         q_codes = []
         q_scales = []
@@ -330,5 +334,4 @@ def tile_cmia_pa_kernel(tc, x_fused, ln_w, ln_b, w_qk, out):
             if unit >= LAG:
                 attention(unit - LAG)
             if unit == 1 or unit == 3:
-                turn_w(Q_BLOCKS[(unit + 3) // 2])
                 quantise_w_block(Q_BLOCKS[(unit + 3) // 2])

@@ -23,8 +23,18 @@ W_ROWS = 256
 K_BLOCKS = (4, 5, 6, 7)
 Q_BLOCKS = (0, 1, 2, 3)
 W_ORDER = K_BLOCKS + Q_BLOCKS
+TURNS = [(b, g) for b in W_ORDER for g in range(PASSES)]
+FIRST_TURNS = 2
 NORMALISED = (0, 2, 1, 3)
 LAG = 2
+
+UNITS = HW // P
+AHEAD = 2
+PIECES = 2
+P_SCALAR = (4, 6, 8, 9, 10, 11, 12, 13, 14, 15)
+A_MOD, A_SCALAR = 3, (0,)
+HELD = 4
+HELD_AT = 5
 
 FLOPS = 2 * CH * 2 * HW * HW + 2 * HW * HW * CH
 
@@ -106,7 +116,7 @@ def tile_cmia_pa_kernel(tc, x_fused, ln_w, ln_b, w_qk, out):
 
         mean_var = keep.tile([P, PACK, 2], F32, name="mean_var")
         rstd = keep.tile([P, PACK], F32, name="rstd")
-        shift = keep.tile([P, 1], F32, name="shift")
+        shift = keep.tile([P, 2], F32, name="shift")
         stats = keep.tile([P, PACK, 2, 6], F32, name="stats")
         y_sb = [keep.tile([P, 4, 2, P], F32, name="y_sb%d" % s) for s in range(PACK)]
 
@@ -129,6 +139,16 @@ def tile_cmia_pa_kernel(tc, x_fused, ln_w, ln_b, w_qk, out):
                 out=rstd[:, s : s + 1], in_=var, func=ACT.Abs_reciprocal_sqrt, bias=eps[:], scale=scale
             )
 
+        def normalise_on_gpsimd(s):
+            nc.gpsimd.tensor_scalar(
+                out=y_sb[s][:],
+                in0=by_parity(s),
+                scalar1=rstd[:, s : s + 1],
+                scalar2=shift[:, s : s + 1],
+                op0=ALU.mult,
+                op1=ALU.add,
+            )
+
         def normalise_on_vector(s):
             nc.vector.tensor_scalar(
                 out=y_sb[s][:],
@@ -149,25 +169,33 @@ def tile_cmia_pa_kernel(tc, x_fused, ln_w, ln_b, w_qk, out):
         nc.scalar.activation(
             out=unused[:], in_=x_sb[1][:], func=ACT.Square, bias=neg_mean[:], scale=1.0, accum_out=x_sq[:]
         )
+        nc.vector.tensor_scalar(
+            out=shift[:, 0:1],
+            in0=mean_var[:, 0, 0:1],
+            scalar1=rstd[:, 0:1],
+            scalar2=-1.0,
+            op0=ALU.mult,
+            op1=ALU.mult,
+        )
+        normalise_on_gpsimd(0)
         half_stats(2, 1)
         join_stats(2)
-        normalise_on_vector(0)
         invert_root(1, x_sq[:], 1.0 / HW)
         invert_root(2, mean_var[:, 2, 1:2], 1.0)
-        nc.scalar.activation(out=shift[:], in_=neg_mean[:], func=ACT.Copy, scale=rstd[:, 1:2])
+        nc.scalar.activation(out=shift[:, 1:2], in_=neg_mean[:], func=ACT.Copy, scale=rstd[:, 1:2])
         half_stats(3, 0)
-        transpose_w(K_BLOCKS[0], 0)
         half_stats(3, 1)
         join_stats(3)
         nc.scalar.activation(
-            out=y_sb[1][:], in_=by_parity(1), func=ACT.Identity, bias=shift[:], scale=rstd[:, 1:2]
+            out=y_sb[1][:], in_=by_parity(1), func=ACT.Identity, bias=shift[:, 1:2], scale=rstd[:, 1:2]
         )
         normalise_on_vector(2)
         invert_root(3, mean_var[:, 3, 1:2], 1.0)
         normalise_on_vector(3)
-        transpose_w(K_BLOCKS[0], 1)
-        group_w(K_BLOCKS[0], 0)
-        group_w(K_BLOCKS[0], 1)
+        for turn in TURNS[:FIRST_TURNS]:
+            transpose_w(*turn)
+            group_w(*turn)
+        quantise_w_block(W_ORDER[0])
 
         gb_ps = psum.tile([P, BANK], F32, tag="bank")
         nc.tensor.transpose(gb_ps[:, 0:P], gb_rows[:].bitcast(F32), ident[:])
@@ -219,19 +247,15 @@ def tile_cmia_pa_kernel(tc, x_fused, ln_w, ln_b, w_qk, out):
                 affine_xn(banks[t], g, t, g == 1 or t % 2 == 0)
             if g == 0:
                 interleave_xn(0, 0, CH)
-                quantise_w_block(K_BLOCKS[0])
                 quantise_xn(0, 0, CH)
-        for b in K_BLOCKS[1:]:
-            for g in range(PASSES):
-                transpose_w(b, g)
-                group_w(b, g)
-        for g in range(PASSES):
-            transpose_w(Q_BLOCKS[0], g)
+        for turn in TURNS[FIRST_TURNS:-HELD]:
+            transpose_w(*turn)
+            group_w(*turn)
         interleave_xn(1, 0, CH // 2)
         interleave_xn(1, CH // 2, CH)
         quantise_xn(1, 0, CH // 2)
         quantise_xn(1, CH // 2, CH)
-        quantise_w_block(K_BLOCKS[1])
+        quantise_w_block(W_ORDER[1])
 
         def project(b, h):
             acc = psum.tile([P, BANK], F32, tag="bank")
@@ -253,10 +277,6 @@ def tile_cmia_pa_kernel(tc, x_fused, ln_w, ln_b, w_qk, out):
         k_codes = [keep.tile([P, BANK], U32, name="k_codes%d" % i, align_bytes=64) for i in range(2)]
         k_scales = [keep.tile([P, BANK], U8, name="k_scales%d" % i, align_bytes=64) for i in range(2)]
 
-        def project_k(i, h, on_scalar):
-            half, first = i // 2, W_ROWS * (i % 2) + P * h
-            copy_out(k_grouped[half][:, first : first + P, :], project(K_BLOCKS[i], h), on_scalar)
-
         def quantise_k(half):
             nc.vector.quantize_mx(
                 out=k_codes[half][:].bitcast(FP8X4),
@@ -264,74 +284,73 @@ def tile_cmia_pa_kernel(tc, x_fused, ln_w, ln_b, w_qk, out):
                 in_=k_grouped[half][:].rearrange("p j s -> p (j s)"),
             )
 
-        def turn_w(b):
-            for g in range(PASSES):
-                transpose_w(b, g)
-                group_w(b, g)
+        q_grouped = [keep.tile([P, P, PACK], BF16, name="q_grouped%d" % i, align_bytes=64) for i in range(UNITS)]
+        q_codes = [keep.tile([P, P], U32, name="q_codes%d" % i, align_bytes=64) for i in range(UNITS)]
+        q_scales = [keep.tile([P, P], U8, name="q_scales%d" % i, align_bytes=64) for i in range(UNITS)]
 
-        project_k(0, 0, False)
-        quantise_w_block(K_BLOCKS[2])
-        project_k(0, 1, True)
-        group_w(Q_BLOCKS[0], 0)
-        project_k(1, 0, False)
-        quantise_w_block(K_BLOCKS[3])
-        project_k(1, 1, True)
-        group_w(Q_BLOCKS[0], 1)
-        project_k(2, 0, False)
-        quantise_k(0)
-        quantise_w_block(Q_BLOCKS[0])
-        project_k(2, 1, True)
-        project_k(3, 0, False)
-        project_k(3, 1, True)
-        for b in Q_BLOCKS[1:]:
-            for g in range(PASSES):
-                transpose_w(b, g)
-                group_w(b, g, b != Q_BLOCKS[2])
-            if b == Q_BLOCKS[1]:
-                quantise_k(1)
-                quantise_w_block(b)
-
-        q_codes = []
-        q_scales = []
-
-        def project_q(unit):
-            b, h = divmod(unit, 2)
-            q_grouped = stage.tile([P, P, PACK], BF16, tag="q_grouped", align_bytes=64)
-            copy_out(q_grouped[:], project(Q_BLOCKS[b], h), unit % 2 == 0)
-            codes_q = stage.tile([P, P], U32, tag="q_codes", align_bytes=64)
-            scales_q = stage.tile([P, P], U8, tag="q_scales", align_bytes=64)
+        def quantise_q(unit):
             nc.vector.quantize_mx(
-                out=codes_q[:].bitcast(FP8X4), scales=scales_q[:], in_=q_grouped[:].rearrange("p j s -> p (j s)")
+                out=q_codes[unit][:].bitcast(FP8X4),
+                scales=q_scales[unit][:],
+                in_=q_grouped[unit][:].rearrange("p j s -> p (j s)"),
             )
-            q_codes.append(codes_q)
-            q_scales.append(scales_q)
 
-        def attention(unit):
-            for half in range(2):
-                att = psum.tile([P, BANK], F32, tag="bank")
-                nc.tensor.matmul_mx(
-                    out=att[:],
-                    lhsT=q_codes[unit][:].bitcast(FP8X4),
-                    lhsT_scale=q_scales[unit][:],
-                    rhs=k_codes[half][:].bitcast(FP8X4),
-                    rhs_scale=k_scales[half][:],
-                    start=True,
-                    stop=True,
-                )
-                att_sb = store.tile([P, BANK], F32, tag="att_sb")
-                if half == 0:
-                    nc.scalar.mul(out=att_sb[:], in_=att[:], mul=HW**-0.5)
+        def attention(unit, half, on_scalar):
+            att = psum.tile([P, BANK], F32, tag="bank")
+            nc.tensor.matmul_mx(
+                out=att[:],
+                lhsT=q_codes[unit][:].bitcast(FP8X4),
+                lhsT_scale=q_scales[unit][:],
+                rhs=k_codes[half][:].bitcast(FP8X4),
+                rhs_scale=k_scales[half][:],
+                start=True,
+                stop=True,
+            )
+            att_sb = store.tile([P, BANK], F32, tag="att_sb")
+            if on_scalar:
+                nc.scalar.mul(out=att_sb[:], in_=att[:], mul=HW**-0.5)
+            else:
+                nc.vector.tensor_scalar_mul(out=att_sb[:], in0=att[:], scalar1=HW**-0.5)
+            nc.sync.dma_start(
+                out=out_rows[P * unit : P * (unit + 1), BANK * half : BANK * (half + 1)], in_=att_sb[:]
+            )
+
+        k_done, q_done = {}, {}
+        pieces = [(unit, half) for unit in range(UNITS) for half in range(2)]
+        waiting = []
+        count = 0
+        steps = [(b, h) for b in W_ORDER for h in range(2)]
+        for i in range(len(steps) + LAG + UNITS):
+            if i < len(steps):
+                b, h = steps[i]
+                if h == 0 and i // 2 + AHEAD < len(W_ORDER):
+                    quantise_w_block(W_ORDER[i // 2 + AHEAD])
+                qk = project(b, h)
+                on_scalar = i in P_SCALAR
+                for todo in waiting:
+                    todo()
+                waiting = []
+                if b in K_BLOCKS:
+                    unit = 2 * K_BLOCKS.index(b) + h
+                    copy_out(k_grouped[unit // 4][:, P * (unit % 4) : P * (unit % 4 + 1), :], qk, on_scalar)
+                    if unit % 4 == 3:
+                        k_done[unit // 4] = i
+                        waiting.append(lambda half=unit // 4: quantise_k(half))
                 else:
-                    nc.vector.tensor_scalar_mul(out=att_sb[:], in0=att[:], scalar1=HW**-0.5)
-                nc.sync.dma_start(
-                    out=out_rows[P * unit : P * (unit + 1), BANK * half : BANK * (half + 1)], in_=att_sb[:]
-                )
-
-        units = HW // P
-        for unit in range(units + LAG):
-            if unit < units:
-                project_q(unit)
-            if unit >= LAG:
-                attention(unit - LAG)
-            if unit == 1 or unit == 3:
-                quantise_w_block(Q_BLOCKS[(unit + 3) // 2])
+                    unit = 2 * Q_BLOCKS.index(b) + h
+                    copy_out(q_grouped[unit][:], qk, on_scalar)
+                    q_done[unit] = i
+                    waiting.append(lambda unit=unit: quantise_q(unit))
+            else:
+                for todo in waiting:
+                    todo()
+                waiting = []
+            ready = [(u, h2) for u, h2 in pieces if u in q_done and h2 in k_done and max(q_done[u], k_done[h2]) + LAG <= i]
+            for piece in ready[:PIECES]:
+                attention(*piece, count % A_MOD in A_SCALAR)
+                count += 1
+                pieces.remove(piece)
+            if i == HELD_AT:
+                for turn in TURNS[-HELD:]:
+                    transpose_w(*turn)
+                    group_w(*turn)

@@ -22,7 +22,8 @@ PASSES = HW // (P * PACK)
 W_ROWS = 256
 K_BLOCKS = (4, 5, 6, 7)
 Q_BLOCKS = (0, 1, 2, 3)
-W_ORDER = K_BLOCKS + Q_BLOCKS
+STEPS = [(b, h) for b in K_BLOCKS + Q_BLOCKS for h in range(2)]
+W_ORDER = [b for i, (b, h) in enumerate(STEPS) if b not in [c for c, g in STEPS[:i]]]
 TURNS = [(b, g) for b in W_ORDER for g in range(PASSES)]
 FIRST_TURNS = 2
 NORMALISED = (0, 2, 1, 3)
@@ -30,11 +31,11 @@ LAG = 2
 
 UNITS = HW // P
 AHEAD = 2
-PIECES = 2
-P_SCALAR = (4, 6, 8, 9, 10, 11, 12, 13, 14, 15)
-A_MOD, A_SCALAR = 3, (0,)
+PIECES = 3
+FIRST_ON_SCALAR = 5
+A_MOD, A_SCALAR = 2, (1,)
 HELD = 4
-HELD_AT = 5
+HELD_AT = 3
 
 FLOPS = 2 * CH * 2 * HW * HW + 2 * HW * HW * CH
 
@@ -149,6 +150,15 @@ def tile_cmia_pa_kernel(tc, x_fused, ln_w, ln_b, w_qk, out):
                 op1=ALU.add,
             )
 
+        def normalise_on_scalar(s, half):
+            nc.scalar.activation(
+                out=y_sb[s][:, 2 * half : 2 * half + 2],
+                in_=by_parity(s)[:, 2 * half : 2 * half + 2],
+                func=ACT.Identity,
+                bias=shift[:, s : s + 1],
+                scale=rstd[:, s : s + 1],
+            )
+
         def normalise_on_vector(s):
             nc.vector.tensor_scalar(
                 out=y_sb[s][:],
@@ -169,6 +179,7 @@ def tile_cmia_pa_kernel(tc, x_fused, ln_w, ln_b, w_qk, out):
         nc.scalar.activation(
             out=unused[:], in_=x_sb[1][:], func=ACT.Square, bias=neg_mean[:], scale=1.0, accum_out=x_sq[:]
         )
+        half_stats(2, 1)
         nc.vector.tensor_scalar(
             out=shift[:, 0:1],
             in0=mean_var[:, 0, 0:1],
@@ -178,7 +189,6 @@ def tile_cmia_pa_kernel(tc, x_fused, ln_w, ln_b, w_qk, out):
             op1=ALU.mult,
         )
         normalise_on_gpsimd(0)
-        half_stats(2, 1)
         join_stats(2)
         invert_root(1, x_sq[:], 1.0 / HW)
         invert_root(2, mean_var[:, 2, 1:2], 1.0)
@@ -186,16 +196,14 @@ def tile_cmia_pa_kernel(tc, x_fused, ln_w, ln_b, w_qk, out):
         half_stats(3, 0)
         half_stats(3, 1)
         join_stats(3)
-        nc.scalar.activation(
-            out=y_sb[1][:], in_=by_parity(1), func=ACT.Identity, bias=shift[:, 1:2], scale=rstd[:, 1:2]
-        )
+        normalise_on_scalar(1, 0)
         normalise_on_vector(2)
         invert_root(3, mean_var[:, 3, 1:2], 1.0)
+        normalise_on_scalar(1, 1)
         normalise_on_vector(3)
         for turn in TURNS[:FIRST_TURNS]:
             transpose_w(*turn)
             group_w(*turn)
-        quantise_w_block(W_ORDER[0])
 
         gb_ps = psum.tile([P, BANK], F32, tag="bank")
         nc.tensor.transpose(gb_ps[:, 0:P], gb_rows[:].bitcast(F32), ident[:])
@@ -246,6 +254,7 @@ def tile_cmia_pa_kernel(tc, x_fused, ln_w, ln_b, w_qk, out):
             for t in range(PACK):
                 affine_xn(banks[t], g, t, g == 1 or t % 2 == 0)
             if g == 0:
+                quantise_w_block(W_ORDER[0])
                 interleave_xn(0, 0, CH)
                 quantise_xn(0, 0, CH)
         for turn in TURNS[FIRST_TURNS:-HELD]:
@@ -319,14 +328,14 @@ def tile_cmia_pa_kernel(tc, x_fused, ln_w, ln_b, w_qk, out):
         pieces = [(unit, half) for unit in range(UNITS) for half in range(2)]
         waiting = []
         count = 0
-        steps = [(b, h) for b in W_ORDER for h in range(2)]
-        for i in range(len(steps) + LAG + UNITS):
-            if i < len(steps):
-                b, h = steps[i]
-                if h == 0 and i // 2 + AHEAD < len(W_ORDER):
-                    quantise_w_block(W_ORDER[i // 2 + AHEAD])
+        for i in range(len(STEPS) + LAG + UNITS):
+            if i < len(STEPS):
+                b, h = STEPS[i]
+                for c in [c for c, g in STEPS[: i + AHEAD + 1] if c not in w_codes]:
+                    if c not in w_codes:
+                        quantise_w_block(c)
                 qk = project(b, h)
-                on_scalar = i in P_SCALAR
+                on_scalar = i >= FIRST_ON_SCALAR
                 for todo in waiting:
                     todo()
                 waiting = []

@@ -25,17 +25,16 @@ Q_BLOCKS = (0, 1, 2, 3)
 STEPS = [(b, h) for b in K_BLOCKS + Q_BLOCKS for h in range(2)]
 W_ORDER = [b for i, (b, h) in enumerate(STEPS) if b not in [c for c, g in STEPS[:i]]]
 TURNS = [(b, g) for b in W_ORDER for g in range(PASSES)]
+ON_VECTOR = TURNS[3:7:2]
 FIRST_TURNS = 2
 NORMALISED = (0, 2, 1, 3)
 LAG = 2
 
 UNITS = HW // P
-AHEAD = 2
+AHEAD = 4
 PIECES = 3
-FIRST_ON_SCALAR = 5
+FIRST_ON_SCALAR = 2
 A_MOD, A_SCALAR = 2, (1,)
-HELD = 4
-HELD_AT = 3
 
 FLOPS = 2 * CH * 2 * HW * HW + 2 * HW * HW * CH
 
@@ -236,6 +235,16 @@ def tile_cmia_pa_kernel(tc, x_fused, ln_w, ln_b, w_qk, out):
                 in_=planes[g][:, :, first:last].rearrange("p t (c i) -> p c t i", i=4),
             )
 
+        def interleave_xn_on_gpsimd(g):
+            nc.gpsimd.tensor_scalar(
+                out=grouped[g][:],
+                in0=planes[g][:].rearrange("p t c -> p c t"),
+                scalar1=1.0,
+                scalar2=0.0,
+                op0=ALU.mult,
+                op1=ALU.add,
+            )
+
         def quantise_xn(g, first, last):
             nc.vector.quantize_mx(
                 out=xn_codes[g][:, first:last].bitcast(FP8X4),
@@ -252,16 +261,16 @@ def tile_cmia_pa_kernel(tc, x_fused, ln_w, ln_b, w_qk, out):
                 for t in range(PACK):
                     transpose_xn(banks[t], g, t, s)
             for t in range(PACK):
-                affine_xn(banks[t], g, t, g == 1 or t % 2 == 0)
+                affine_xn(banks[t], g, t, t % 2 == 0)
             if g == 0:
-                quantise_w_block(W_ORDER[0])
-                interleave_xn(0, 0, CH)
-                quantise_xn(0, 0, CH)
-        for turn in TURNS[FIRST_TURNS:-HELD]:
+                interleave_xn_on_gpsimd(0)
+        for turn in TURNS[FIRST_TURNS:]:
             transpose_w(*turn)
-            group_w(*turn)
+            group_w(*turn, turn not in ON_VECTOR)
         interleave_xn(1, 0, CH // 2)
         interleave_xn(1, CH // 2, CH)
+        quantise_w_block(W_ORDER[0])
+        quantise_xn(0, 0, CH)
         quantise_xn(1, 0, CH // 2)
         quantise_xn(1, CH // 2, CH)
         quantise_w_block(W_ORDER[1])
@@ -359,7 +368,3 @@ def tile_cmia_pa_kernel(tc, x_fused, ln_w, ln_b, w_qk, out):
                 attention(*piece, count % A_MOD in A_SCALAR)
                 count += 1
                 pieces.remove(piece)
-            if i == HELD_AT:
-                for turn in TURNS[-HELD:]:
-                    transpose_w(*turn)
-                    group_w(*turn)

@@ -31,9 +31,8 @@ NORMALISED = (0, 2, 1, 3)
 LAG = 2
 
 UNITS = HW // P
-AHEAD = 4
 PIECES = 3
-FIRST_ON_SCALAR = 2
+FIRST_ON_SCALAR = 3
 A_MOD, A_SCALAR = 2, (1,)
 
 FLOPS = 2 * CH * 2 * HW * HW + 2 * HW * HW * CH
@@ -66,7 +65,9 @@ def tile_cmia_pa_kernel(tc, x_fused, ln_w, ln_b, w_qk, out):
         x_sb = []
         for s in range(PACK):
             x_s = keep.tile([P, HW], BF16, name="x_sb%d" % s)
-            nc.sync.dma_start(out=x_s[:], in_=x_rows[:, s, :])
+            step = BANK if s == 0 else HW
+            for first in range(0, HW, step):
+                nc.sync.dma_start(out=x_s[:, first : first + step], in_=x_rows[:, s, first : first + step])
             x_sb.append(x_s)
         w_sb = {}
         for b in W_ORDER:
@@ -200,9 +201,10 @@ def tile_cmia_pa_kernel(tc, x_fused, ln_w, ln_b, w_qk, out):
         invert_root(3, mean_var[:, 3, 1:2], 1.0)
         normalise_on_scalar(1, 1)
         normalise_on_vector(3)
-        for turn in TURNS[:FIRST_TURNS]:
-            transpose_w(*turn)
-            group_w(*turn)
+        for n in range(FIRST_TURNS):
+            transpose_w(*TURNS[n])
+            group_w(*TURNS[n], n == 0)
+        quantise_w_block(W_ORDER[0])
 
         gb_ps = psum.tile([P, BANK], F32, tag="bank")
         nc.tensor.transpose(gb_ps[:, 0:P], gb_rows[:].bitcast(F32), ident[:])
@@ -269,7 +271,6 @@ def tile_cmia_pa_kernel(tc, x_fused, ln_w, ln_b, w_qk, out):
             group_w(*turn, turn not in ON_VECTOR)
         interleave_xn(1, 0, CH // 2)
         interleave_xn(1, CH // 2, CH)
-        quantise_w_block(W_ORDER[0])
         quantise_xn(0, 0, CH)
         quantise_xn(1, 0, CH // 2)
         quantise_xn(1, CH // 2, CH)
@@ -333,6 +334,11 @@ def tile_cmia_pa_kernel(tc, x_fused, ln_w, ln_b, w_qk, out):
                 out=out_rows[P * unit : P * (unit + 1), BANK * half : BANK * (half + 1)], in_=att_sb[:]
             )
 
+        def quantise_ahead(step):
+            for c, g in STEPS[: step + 1]:
+                if c not in w_codes:
+                    quantise_w_block(c)
+
         k_done, q_done = {}, {}
         pieces = [(unit, half) for unit in range(UNITS) for half in range(2)]
         waiting = []
@@ -340,14 +346,15 @@ def tile_cmia_pa_kernel(tc, x_fused, ln_w, ln_b, w_qk, out):
         for i in range(len(STEPS) + LAG + UNITS):
             if i < len(STEPS):
                 b, h = STEPS[i]
-                for c in [c for c, g in STEPS[: i + AHEAD + 1] if c not in w_codes]:
-                    if c not in w_codes:
-                        quantise_w_block(c)
+                if i < 8:
+                    quantise_ahead(i + 4)
                 qk = project(b, h)
                 on_scalar = i >= FIRST_ON_SCALAR
                 for todo in waiting:
                     todo()
                 waiting = []
+                if i >= 8:
+                    quantise_ahead(i + 3)
                 if b in K_BLOCKS:
                     unit = 2 * K_BLOCKS.index(b) + h
                     copy_out(k_grouped[unit // 4][:, P * (unit % 4) : P * (unit % 4 + 1), :], qk, on_scalar)

from contextlib import ExitStack

import concourse.mybir as mybir
from concourse.masks import make_identity

F32 = mybir.dt.float32
BF16 = mybir.dt.bfloat16
U32 = mybir.dt.uint32
U8 = mybir.dt.uint8
FP8X4 = mybir.dt.float8_e4m3fn_x4
ACT = mybir.ActivationFunctionType
ALU = mybir.AluOpType

P = 128
PACK = 4
BANK = 512
BANKS = 8
CH = 512
HW = 1024
EPS = 1e-5
PASSES = HW // (P * PACK)
W_ROWS = 256
K_BLOCKS = (4, 5, 6, 7)
Q_BLOCKS = (0, 1, 2, 3)
STEPS = [(b, h) for b in K_BLOCKS + Q_BLOCKS for h in range(2)]
W_ORDER = [b for i, (b, h) in enumerate(STEPS) if b not in [c for c, g in STEPS[:i]]]
TURNS = [(b, g) for b in W_ORDER for g in range(PASSES)]
ON_VECTOR = TURNS[3:7:2]
FIRST_TURNS = 2
NORMALISED = (0, 2, 1, 3)
LAG = 2

UNITS = HW // P
PIECES = 3
FIRST_ON_SCALAR = 3
A_MOD, A_SCALAR = 2, (1,)

FLOPS = 2 * CH * 2 * HW * HW + 2 * HW * HW * CH


def tile_cmia_pa_kernel(tc, x_fused, ln_w, ln_b, w_qk, out):
    nc = tc.nc
    x_rows = x_fused.flatten_outer_dims().rearrange("(m s) n -> m s n", s=PACK)
    w_blocks = w_qk.rearrange("(b j a) n -> b j (a n)", j=P, a=2)
    out_rows = out.flatten_outer_dims()

    with ExitStack() as ctx:
        ctx.enter_context(tc.manual_schedule())
        keep = ctx.enter_context(tc.tile_pool(name="keep", bufs=1))
        stage = ctx.enter_context(tc.tile_pool(name="stage", bufs=8))
        store = ctx.enter_context(tc.tile_pool(name="store", bufs=16))
        psum = ctx.enter_context(tc.psum_pool(name="psum", bufs=BANKS))

        gb_rows = keep.tile([P, 2 * P], BF16, name="gb_rows")
        nc.vector.memset(gb_rows[:], 0.0)
        nc.scalar.dma_start(out=gb_rows[0:4, :], in_=ln_w.rearrange("(r w) -> r w", r=4))
        nc.scalar.dma_start(out=gb_rows[4:8, :], in_=ln_b.rearrange("(r w) -> r w", r=4))
        eps = keep.tile([P, 1], F32, name="eps")
        nc.vector.memset(eps[:], EPS)
        first_root = keep.tile([P, 1], F32, name="first_root")
        nc.scalar.activation(out=first_root[:], in_=eps[:], func=ACT.Abs_reciprocal_sqrt)
        ident = keep.tile([P, P], F32, name="ident")
        make_identity(nc, ident[:])

        x_sb = []
        for s in range(PACK):
            x_s = keep.tile([P, HW], BF16, name="x_sb%d" % s)
            step = BANK if s == 0 else HW
            for first in range(0, HW, step):
                nc.sync.dma_start(out=x_s[:, first : first + step], in_=x_rows[:, s, first : first + step])
            x_sb.append(x_s)
        w_sb = {}
        for b in W_ORDER:
            w_b = keep.tile([P, 2 * HW], BF16, name="w_sb%d" % b)
            nc.sync.dma_start(out=w_b[:], in_=w_blocks[b])
            w_sb[b] = w_b

        w_grouped = {}
        w_codes = {}
        w_scales = {}

        def copy_out(dst, src, on_scalar):
            if on_scalar:
                nc.scalar.copy(out=dst, in_=src)
            else:
                nc.vector.tensor_copy(out=dst, in_=src)

        w_banks = {}

        def transpose_w(b, g):
            words = w_sb[b][:].bitcast(F32)
            wt = psum.tile([P, BANK], F32, tag="bank")
            for a in range(2):
                for u in range(2):
                    first = 512 * a + 256 * g + P * u
                    nc.tensor.transpose(
                        wt[:, (2 * a + u) * P : (2 * a + u + 1) * P], words[:, first : first + P], ident[:]
                    )
            w_banks[b, g] = wt

        def group_w(b, g, on_scalar=True):
            if g == 0:
                w_grouped[b] = keep.tile([P, PASSES * W_ROWS * PACK], BF16, name="w_grouped%d" % b, align_bytes=64)
            grouped_words = w_grouped[b][:].bitcast(F32)[:, BANK * g : BANK * (g + 1)]
            copy_out(
                grouped_words.rearrange("p (j a u) -> p j a u", a=2, u=2),
                w_banks[b, g][:].rearrange("p (a u j) -> p j a u", a=2, u=2),
                on_scalar,
            )

        def quantise_w_block(b):
            codes_w = keep.tile([P, PASSES * W_ROWS], U32, name="w_codes%d" % b, align_bytes=64)
            scales_w = keep.tile([P, PASSES * W_ROWS], U8, name="w_scales%d" % b, align_bytes=64)
            nc.vector.quantize_mx(out=codes_w[:].bitcast(FP8X4), scales=scales_w[:], in_=w_grouped[b][:])
            w_codes[b] = codes_w
            w_scales[b] = scales_w

        mean_var = keep.tile([P, PACK, 2], F32, name="mean_var")
        rstd = keep.tile([P, PACK], F32, name="rstd")
        shift = keep.tile([P, 2], F32, name="shift")
        stats = keep.tile([P, PACK, 2, 6], F32, name="stats")
        y_sb = [keep.tile([P, 4, 2, P], F32, name="y_sb%d" % s) for s in range(PACK)]

        def by_parity(s):
            return x_sb[s][:].rearrange("p (r q e) -> p r e q", q=P, e=2)

        x_sum = keep.tile([P, 1], F32, name="x_sum")
        x_sq = keep.tile([P, 1], F32, name="x_sq")
        neg_mean = keep.tile([P, 1], F32, name="neg_mean")
        unused = keep.tile([P, HW], BF16, name="unused")

        def half_stats(s, half):
            nc.vector.bn_stats(out=stats[:, s, half, :], in_=x_sb[s][:, BANK * half : BANK * (half + 1)])

        def join_stats(s):
            nc.vector.bn_aggr(out=mean_var[:, s, :], in_=stats[:, s, :, :].rearrange("p h d -> p (h d)"))

        def invert_root(s, var, scale):
            nc.scalar.activation(
                out=rstd[:, s : s + 1], in_=var, func=ACT.Abs_reciprocal_sqrt, bias=eps[:], scale=scale
            )

        def normalise_on_gpsimd(s):
            nc.gpsimd.tensor_scalar(
                out=y_sb[s][:],
                in0=by_parity(s),
                scalar1=rstd[:, s : s + 1],
                scalar2=shift[:, s : s + 1],
                op0=ALU.mult,
                op1=ALU.add,
            )

        def normalise_on_scalar(s, half):
            nc.scalar.activation(
                out=y_sb[s][:, 2 * half : 2 * half + 2],
                in_=by_parity(s)[:, 2 * half : 2 * half + 2],
                func=ACT.Identity,
                bias=shift[:, s : s + 1],
                scale=rstd[:, s : s + 1],
            )

        def normalise_on_vector(s):
            nc.vector.tensor_scalar(
                out=y_sb[s][:],
                in0=by_parity(s),
                scalar1=mean_var[:, s, 0:1],
                scalar2=rstd[:, s : s + 1],
                op0=ALU.subtract,
                op1=ALU.mult,
            )

        half_stats(0, 0)
        nc.scalar.activation(out=unused[:], in_=x_sb[1][:], func=ACT.Identity, accum_out=x_sum[:])
        half_stats(0, 1)
        join_stats(0)
        nc.scalar.mul(out=neg_mean[:], in_=x_sum[:], mul=-1.0 / HW)
        invert_root(0, mean_var[:, 0, 1:2], 1.0)
        half_stats(2, 0)
        nc.scalar.activation(
            out=unused[:], in_=x_sb[1][:], func=ACT.Square, bias=neg_mean[:], scale=1.0, accum_out=x_sq[:]
        )
        half_stats(2, 1)
        nc.vector.tensor_scalar(
            out=shift[:, 0:1],
            in0=mean_var[:, 0, 0:1],
            scalar1=rstd[:, 0:1],
            scalar2=-1.0,
            op0=ALU.mult,
            op1=ALU.mult,
        )
        normalise_on_gpsimd(0)
        join_stats(2)
        invert_root(1, x_sq[:], 1.0 / HW)
        invert_root(2, mean_var[:, 2, 1:2], 1.0)
        nc.scalar.activation(out=shift[:, 1:2], in_=neg_mean[:], func=ACT.Copy, scale=rstd[:, 1:2])
        half_stats(3, 0)
        half_stats(3, 1)
        join_stats(3)
        normalise_on_scalar(1, 0)
        normalise_on_vector(2)
        invert_root(3, mean_var[:, 3, 1:2], 1.0)
        normalise_on_scalar(1, 1)
        normalise_on_vector(3)
        for n in range(FIRST_TURNS):
            transpose_w(*TURNS[n])
            group_w(*TURNS[n], n == 0)
        quantise_w_block(W_ORDER[0])

        gb_ps = psum.tile([P, BANK], F32, tag="bank")
        nc.tensor.transpose(gb_ps[:, 0:P], gb_rows[:].bitcast(F32), ident[:])
        gb = keep.tile([P, 16], F32, name="gb")
        nc.scalar.copy(out=gb[:], in_=gb_ps[:].bitcast(BF16)[:, 0:16])


        xn_codes = [keep.tile([P, CH], U32, name="xn_codes%d" % g, align_bytes=64) for g in range(PASSES)]
        xn_scales = [keep.tile([P, CH], U8, name="xn_scales%d" % g, align_bytes=64) for g in range(PASSES)]
        planes = [keep.tile([P, PACK, CH], BF16, name="xn_planes%d" % g) for g in range(PASSES)]
        grouped = [keep.tile([P, CH, PACK], BF16, name="xn_grouped%d" % g, align_bytes=64) for g in range(PASSES)]

        def transpose_xn(bank, g, t, s):
            u, e = divmod(t, 2)
            nc.tensor.transpose(bank[:, s * P : (s + 1) * P], y_sb[s][:, 2 * g + u, e, :], ident[:])

        def affine_xn(bank, g, t, on_scalar):
            col = PACK * g + t
            gain, bias = gb[:, col : col + 1], gb[:, 8 + col : 9 + col]
            if on_scalar:
                nc.scalar.activation(out=planes[g][:, t, :], in_=bank[:], func=ACT.Identity, bias=bias, scale=gain)
            else:
                nc.vector.tensor_scalar(
                    out=planes[g][:, t, :], in0=bank[:], scalar1=gain, scalar2=bias, op0=ALU.mult, op1=ALU.add
                )

        def interleave_xn(g, first, last):
            nc.vector.tensor_copy(
                out=grouped[g][:, first:last, :].rearrange("p (c i) t -> p c t i", i=4),
                in_=planes[g][:, :, first:last].rearrange("p t (c i) -> p c t i", i=4),
            )

        def interleave_xn_on_gpsimd(g):
            nc.gpsimd.tensor_scalar(
                out=grouped[g][:],
                in0=planes[g][:].rearrange("p t c -> p c t"),
                scalar1=1.0,
                scalar2=0.0,
                op0=ALU.mult,
                op1=ALU.add,
            )

        def quantise_xn(g, first, last):
            nc.vector.quantize_mx(
                out=xn_codes[g][:, first:last].bitcast(FP8X4),
                scales=xn_scales[g][:, first:last],
                in_=grouped[g][:, first:last, :].rearrange("p c t -> p (c t)"),
            )

        for g in range(PASSES):
            banks = []
            for t in range(PACK):
                xt = psum.tile([P, BANK], F32, tag="bank")
                banks.append(xt)
            for s in NORMALISED:
                for t in range(PACK):
                    transpose_xn(banks[t], g, t, s)
            for t in range(PACK):
                affine_xn(banks[t], g, t, t % 2 == 0)
            if g == 0:
                interleave_xn_on_gpsimd(0)
        for turn in TURNS[FIRST_TURNS:]:
            transpose_w(*turn)
            group_w(*turn, turn not in ON_VECTOR)
        interleave_xn(1, 0, CH // 2)
        interleave_xn(1, CH // 2, CH)
        quantise_xn(0, 0, CH)
        quantise_xn(1, 0, CH // 2)
        quantise_xn(1, CH // 2, CH)
        quantise_w_block(W_ORDER[1])

        def project(b, h):
            acc = psum.tile([P, BANK], F32, tag="bank")
            for s in range(PACK):
                for g in range(PASSES):
                    cols = slice(W_ROWS * g + P * h, W_ROWS * g + P * (h + 1))
                    nc.tensor.matmul_mx(
                        out=acc[:, s * P : (s + 1) * P],
                        lhsT=xn_codes[g][:, s * P : (s + 1) * P].bitcast(FP8X4),
                        lhsT_scale=xn_scales[g][:, s * P : (s + 1) * P],
                        rhs=w_codes[b][:, cols].bitcast(FP8X4),
                        rhs_scale=w_scales[b][:, cols],
                        start=(g == 0),
                        stop=(g == PASSES - 1),
                    )
            return acc[:].rearrange("p (s j) -> p j s", s=PACK)

        k_grouped = [keep.tile([P, BANK, PACK], BF16, name="k_grouped%d" % i, align_bytes=64) for i in range(2)]
        k_codes = [keep.tile([P, BANK], U32, name="k_codes%d" % i, align_bytes=64) for i in range(2)]
        k_scales = [keep.tile([P, BANK], U8, name="k_scales%d" % i, align_bytes=64) for i in range(2)]

        def quantise_k(half):
            nc.vector.quantize_mx(
                out=k_codes[half][:].bitcast(FP8X4),
                scales=k_scales[half][:],
                in_=k_grouped[half][:].rearrange("p j s -> p (j s)"),
            )

        q_grouped = [keep.tile([P, P, PACK], BF16, name="q_grouped%d" % i, align_bytes=64) for i in range(UNITS)]
        q_codes = [keep.tile([P, P], U32, name="q_codes%d" % i, align_bytes=64) for i in range(UNITS)]
        q_scales = [keep.tile([P, P], U8, name="q_scales%d" % i, align_bytes=64) for i in range(UNITS)]

        def quantise_q(unit):
            nc.vector.quantize_mx(
                out=q_codes[unit][:].bitcast(FP8X4),
                scales=q_scales[unit][:],
                in_=q_grouped[unit][:].rearrange("p j s -> p (j s)"),
            )

        def attention(unit, half, on_scalar):
            att = psum.tile([P, BANK], F32, tag="bank")
            nc.tensor.matmul_mx(
                out=att[:],
                lhsT=q_codes[unit][:].bitcast(FP8X4),
                lhsT_scale=q_scales[unit][:],
                rhs=k_codes[half][:].bitcast(FP8X4),
                rhs_scale=k_scales[half][:],
                start=True,
                stop=True,
            )
            att_sb = store.tile([P, BANK], F32, tag="att_sb")
            if on_scalar:
                nc.scalar.mul(out=att_sb[:], in_=att[:], mul=HW**-0.5)
            else:
                nc.vector.tensor_scalar_mul(out=att_sb[:], in0=att[:], scalar1=HW**-0.5)
            nc.sync.dma_start(
                out=out_rows[P * unit : P * (unit + 1), BANK * half : BANK * (half + 1)], in_=att_sb[:]
            )

        def quantise_ahead(step):
            for c, g in STEPS[: step + 1]:
                if c not in w_codes:
                    quantise_w_block(c)

        k_done, q_done = {}, {}
        pieces = [(unit, half) for unit in range(UNITS) for half in range(2)]
        waiting = []
        count = 0
        for i in range(len(STEPS) + LAG + UNITS):
            if i < len(STEPS):
                b, h = STEPS[i]
                if i < 8:
                    quantise_ahead(i + 4)
                qk = project(b, h)
                on_scalar = i >= FIRST_ON_SCALAR
                for todo in waiting:
                    todo()
                waiting = []
                if i >= 8:
                    quantise_ahead(i + 3)
                if b in K_BLOCKS:
                    unit = 2 * K_BLOCKS.index(b) + h
                    copy_out(k_grouped[unit // 4][:, P * (unit % 4) : P * (unit % 4 + 1), :], qk, on_scalar)
                    if unit % 4 == 3:
                        k_done[unit // 4] = i
                        waiting.append(lambda half=unit // 4: quantise_k(half))
                else:
                    unit = 2 * Q_BLOCKS.index(b) + h
                    copy_out(q_grouped[unit][:], qk, on_scalar)
                    q_done[unit] = i
                    waiting.append(lambda unit=unit: quantise_q(unit))
            else:
                for todo in waiting:
                    todo()
                waiting = []
            ready = [(u, h2) for u, h2 in pieces if u in q_done and h2 in k_done and max(q_done[u], k_done[h2]) + LAG <= i]
            for piece in ready[:PIECES]:
                attention(*piece, count % A_MOD in A_SCALAR)
                count += 1
                pieces.remove(piece)
